import numpy as np
import ml_dtypes


def mxq(x, axis, fmt="e4m3"):
    dtype, down = {"e4m3": (ml_dtypes.float8_e4m3fn, 7), "e5m2": (ml_dtypes.float8_e5m2, 14)}[fmt]
    v = np.moveaxis(np.asarray(x, np.float32).astype(ml_dtypes.bfloat16).astype(np.float64), axis, -1)
    blocks = v.reshape(v.shape[:-1] + (-1, 32))
    amax = np.abs(blocks).max(-1, keepdims=True)
    byte = np.maximum(np.where(amax > 0, np.frexp(amax)[1] - 1 + 127, 0) - down, 1)
    scale = np.exp2(byte - 127.0)
    codes = (blocks / scale).astype(np.float32).astype(dtype).astype(np.float64)
    return np.moveaxis((codes * scale).reshape(v.shape), -1, axis)


WIDE = False


def mx_kscale(k):
    if not WIDE:
        return np.ones(k)
    levels = np.array([10, -10, 5, -5, 0])
    if k % 512:
        return np.exp2(np.random.permutation(np.resize(levels, k // 32))).repeat(32)
    a = np.empty((k // 512, 16))
    for p in range(k // 512):
        a[p, :8] = np.random.permutation(np.resize(levels, 8))
        for g in range(8):
            far = levels[np.abs(levels - a[p, g]) >= 10]
            a[p, g + 8] = far[np.random.randint(len(far))]
    return np.exp2(a.ravel()).repeat(32)


BF16 = ml_dtypes.bfloat16


def bf(x):
    return np.asarray(x, np.float32).astype(BF16)


def f64(x):
    return np.asarray(x).astype(np.float64)


B, T, D, H = 8, 128, 1024, 1024


def sigmoid(v):
    return 1.0 / (1.0 + np.exp(-v))


def setup_inputs():
    s = mx_kscale(D)
    return {"x": bf(np.random.standard_normal((B, T, D)) * s),
            "Wq": bf(np.random.standard_normal((H, D)) * 1.0 / np.sqrt(D) / s),
            "bq": bf(np.random.standard_normal(H) * 0.5),
            "Wk": bf(np.random.standard_normal((H, D)) * 0.6 / np.sqrt(D) / s),
            "bk": bf(np.random.standard_normal(H) * 0.3),
            "Wv": bf(np.random.standard_normal((H, D)) * 2.0 / np.sqrt(D) / s),
            "bv": bf(np.random.standard_normal(H) * 0.5),
            "wbias": bf(np.random.uniform(0.0, 1.0, H))}


def reference(x, Wq, bq, Wk, bk, Wv, bv, wbias):
    xq = mxq(f64(x), 2, "e4m3")
    Q = (xq @ mxq(f64(Wq), 1, "e4m3").T) + f64(bq)
    K = (xq @ mxq(f64(Wk), 1, "e4m3").T) + f64(bk)
    V = (xq @ mxq(f64(Wv), 1, "e4m3").T) + f64(bv)
    Q_sig = sigmoid(Q)
    numer = np.exp(K + f64(wbias))
    denom = numer.sum(axis=0)
    weighted = (numer * V).sum(axis=0) / denom
    Yt = Q_sig * weighted
    return Yt

@@ -1,0 +1,318 @@
+from contextlib import ExitStack
+
+import concourse.mybir as mybir
+from concourse.masks import make_identity
+
+FLOPS = 2 * 1024 * 1024 * 3072
+
+F32 = mybir.dt.float32
+BF16 = mybir.dt.bfloat16
+U32 = mybir.dt.uint32
+U8 = mybir.dt.uint8
+FP8X4 = mybir.dt.float8_e4m3fn_x4
+ACT = mybir.ActivationFunctionType
+ALU = mybir.AluOpType
+
+P = 128
+B = 8
+D = 1024
+H = 1024
+CH = 256
+NCH = H // CH
+PINNED = True
+PSUM_ON_G = True
+
+
+def tile_aftattention_kernel(tc, x, Wq, bq, Wk, bk, Wv, bv, wbias, out):
+    nc = tc.nc
+    with ExitStack() as ctx:
+        const = ctx.enter_context(tc.tile_pool(name="const", bufs=1))
+        gwp = ctx.enter_context(tc.tile_pool(name="gwp", bufs=4))
+        nump = ctx.enter_context(tc.tile_pool(name="nump", bufs=8))
+        prodp = ctx.enter_context(tc.tile_pool(name="prodp", bufs=6))
+        accp = ctx.enter_context(tc.tile_pool(name="accp", bufs=2))
+        thp = ctx.enter_context(tc.tile_pool(name="thp", bufs=12))
+        outp = ctx.enter_context(tc.tile_pool(name="outp", bufs=4))
+        trp = ctx.enter_context(tc.psum_pool(name="trp", bufs=2))
+        otp = ctx.enter_context(tc.psum_pool(name="otp", bufs=2))
+        mxp = ctx.enter_context(tc.psum_pool(name="mxp", bufs=4))
+        tpools = {"tr": trp, "ot": otp}
+        if PINNED:
+            ctx.enter_context(tc.manual_schedule())
+
+        ident = const.tile([P, P], F32, name="ident")
+        make_identity(nc, ident[:])
+        identb = const.tile([P, P], BF16, name="identb")
+        brow = const.tile([P, P], BF16, name="brow")
+        bvb = const.tile([P, H], BF16, name="bvb")
+        warm = const.tile([P, 1], F32, name="warm")
+        warm2 = const.tile([P, 1], F32, name="warm2")
+        bqh = const.tile([P, 8], F32, name="bqh")
+        nc.vector.memset(warm[:], 0.0)
+        nc.scalar.activation(out=warm2[:], in_=warm[:], func=ACT.Exp)
+        nc.vector.memset(brow[:], 0.0)
+        nc.scalar.dma_start(out=brow[0:8, :], in_=bq.rearrange("(i p) -> i p", p=P))
+
+        x_raw = const.tile([P, B * D], BF16, name="x_raw")
+        x_raw3 = x_raw[:].rearrange("p (b k) -> p b k", b=B)
+        x_t = x.rearrange("b t k -> t b k")
+        w_dram = {"k": Wk, "v": Wv, "q": Wq}
+        w_raw = {}
+
+        def load_x(j):
+            nc.sync.dma_start(out=x_raw3[:, 2 * j:2 * j + 2, :], in_=x_t[:, 2 * j:2 * j + 2, :])
+
+        def load_w(w, c):
+            t = const.tile([P, 2 * D], BF16, name="wraw_%s%d" % (w, c))
+            nc.sync.dma_start(
+                out=t[:].rearrange("p (i k) -> p i k", i=2),
+                in_=w_dram[w][c * CH:(c + 1) * CH, :].rearrange("(i p) k -> p i k", p=P),
+            )
+            w_raw[(w, c)] = t
+
+        nc.sync.dma_start(out=x_raw3[:, 0:1, :], in_=x_t[:, 0:1, :])
+        nc.sync.dma_start(out=x_raw3[:, 1:2, :], in_=x_t[:, 1:2, :])
+        load_w("k", 0)
+        load_w("v", 0)
+        load_x(1)
+        load_x(2)
+        load_x(3)
+        load_w("q", 0)
+        for c in range(1, NCH):
+            for w in ("k", "v", "q"):
+                load_w(w, c)
+            if c == 1:
+                nc.sync.dma_start(out=bvb[:], in_=bv.partition_broadcast(P))
+
+        nc.vector.tensor_copy(out=identb[:], in_=ident[:])
+
+        def bias_stage():
+            bt = trp.tile([P, P], BF16, name="bt", tag="tr")
+            nc.tensor.transpose(out=bt[:], in_=brow[:], identity=identb[:])
+            nc.vector.tensor_scalar_mul(out=bqh[:], in0=bt[:, 0:8], scalar1=0.5)
+
+        xw = x_raw[:].bitcast(F32)
+        gx = [const.tile([P, 2048], F32, name="gx%d" % h, align_bytes=64) for h in range(2)]
+        xc = [const.tile([P, 1024], U32, name="xc%d" % h, align_bytes=64) for h in range(2)]
+        xs = [const.tile([P, 1024], U8, name="xs%d" % h, align_bytes=64) for h in range(2)]
+
+        def transpose_bank(words, first_col, tag):
+            bank = tpools[tag].tile([P, 4, P], F32, name="trb", tag=tag)
+            for j in range(4):
+                nc.tensor.transpose(out=bank[:, j, :],
+                                    in_=words[:, first_col + 256 * (j // 2) + j % 2:first_col + 256 * (j // 2 + 1):2],
+                                    identity=ident[:])
+            return bank[:].rearrange("p (g u) r -> p g r u", g=2, u=2)
+
+        def evac(eng, dst, src):
+            if eng == "V":
+                nc.vector.tensor_copy(out=dst, in_=src)
+            else:
+                nc.scalar.copy(out=dst, in_=src)
+
+        def trx(b, tag, eng):
+            src = transpose_bank(xw, b * 512, tag)
+            dst = gx[b // 4][:].rearrange("p (g b r u) -> p g b r u", g=2, b=4, r=P, u=2)[:, :, b % 4, :, :]
+            evac(eng, dst, src)
+
+        def qx(pb):
+            h = pb // 2
+            for g in range(2):
+                w0 = g * 512 + (pb % 2) * 256
+                nc.vector.quantize_mx(out=xc[h][:, w0:w0 + 256].bitcast(FP8X4), scales=xs[h][:, w0:w0 + 256],
+                                      in_=gx[h][:, 2 * w0:2 * w0 + 512].bitcast(BF16))
+
+        wc = {}
+        ws = {}
+        gws = {}
+
+        def trw(w, c, i, eng="S", tag="tr"):
+            if i == 0:
+                gw_new = gwp.tile([P, 1024], F32, name="gw", tag="gw", align_bytes=64)
+                gws[(w, c)] = gw_new
+            src = transpose_bank(w_raw[(w, c)][:].bitcast(F32), i * 512, tag)
+            dst = gws[(w, c)][:].rearrange("p (g i r u) -> p g i r u", g=2, i=2, r=P, u=2)[:, :, i, :, :]
+            evac(eng, dst, src)
+
+        def tq(w, c):
+            codes = const.tile([P, 512], U32, name="wc_%s%d" % (w, c), align_bytes=64)
+            scales = const.tile([P, 512], U8, name="ws_%s%d" % (w, c), align_bytes=64)
+            nc.vector.quantize_mx(out=codes[:].bitcast(FP8X4), scales=scales[:],
+                                  in_=gws[(w, c)][:].bitcast(BF16))
+            wc[(w, c)] = codes
+            ws[(w, c)] = scales
+
+        def kv_bank(w, c, pb):
+            bank = mxp.tile([P, 2, CH], F32, name="kvb", tag="mx")
+            for bb in range(2):
+                b = 2 * pb + bb
+                h = b // 4
+                for g in range(2):
+                    xcols = slice(g * 512 + (b % 4) * P, g * 512 + (b % 4) * P + P)
+                    wcols = slice(g * CH, (g + 1) * CH)
+                    nc.tensor.matmul_mx(out=bank[:, bb, :],
+                                        lhsT=xc[h][:, xcols].bitcast(FP8X4), lhsT_scale=xs[h][:, xcols],
+                                        rhs=wc[(w, c)][:, wcols].bitcast(FP8X4), rhs_scale=ws[(w, c)][:, wcols],
+                                        start=(g == 0), stop=(g == 1))
+            return bank
+
+        st = {}
+
+        def chain(eng, c, key, tiles, pb):
+            if pb == 1:
+                acc = accp.tile([P, 2, CH], F32, name=key, tag=key)
+                st[(key, c)] = acc
+                eng.tensor_tensor(out=acc[:], in0=tiles[0][:], in1=tiles[1][:], op=ALU.add)
+            elif pb > 1:
+                acc = st[(key, c)]
+                eng.tensor_tensor(out=acc[:], in0=acc[:], in1=tiles[pb][:], op=ALU.add)
+            if pb == 3:
+                acc = st[(key, c)]
+                tot = accp.tile([P, CH], F32, name=key + "_t", tag=key + "_t")
+                eng.tensor_tensor(out=tot[:], in0=acc[:, 0, :], in1=acc[:, 1, :], op=ALU.add)
+                st[(key + "_t", c)] = tot
+
+        def kb(c, pb):
+            bank = kv_bank("k", c, pb)
+            n = nump.tile([P, 2, CH], F32, name="numer", tag="numer")
+            nc.scalar.activation(out=n[:], in_=bank[:], func=ACT.Exp)
+            if pb == 0:
+                st[("numer", c)] = {}
+            st[("numer", c)][pb] = n
+            chain(nc.gpsimd, c, "acc_n", st[("numer", c)], pb)
+
+        def vb(c, pb):
+            bank = kv_bank("v", c, pb)
+            pr = prodp.tile([P, 2, CH], F32, name="prod", tag="prod")
+            nc.vector.tensor_tensor(out=pr[:], in0=bank[:], in1=st[("numer", c)][pb][:], op=ALU.mult)
+            if pb == 0:
+                st[("prod", c)] = {}
+            st[("prod", c)][pb] = pr
+            p_eng = nc.gpsimd if PSUM_ON_G else nc.vector
+            chain(p_eng, c, "acc_p", st[("prod", c)], pb)
+
+        def qb(c, i, h):
+            bank = mxp.tile([P, 512], F32, name="qbank", tag="mx")
+            for g in range(2):
+                wcols = slice(g * CH + i * P, g * CH + (i + 1) * P)
+                xcols = slice(g * 512, (g + 1) * 512)
+                nc.tensor.matmul_mx(out=bank[:],
+                                    lhsT=wc[("q", c)][:, wcols].bitcast(FP8X4), lhsT_scale=ws[("q", c)][:, wcols],
+                                    rhs=xc[h][:, xcols].bitcast(FP8X4), rhs_scale=xs[h][:, xcols],
+                                    start=(g == 0), stop=(g == 1))
+            t = thp.tile([P, 512], F32, name="th", tag="th")
+            nc.scalar.activation(out=t[:], in_=bank[:], func=ACT.Tanh,
+                                 bias=bqh[:, 2 * c + i:2 * c + i + 1], scale=0.5)
+            st[("th", c, i, h)] = t
+
+        def q4(c):
+            for i, h in ((0, 0), (1, 0), (0, 1), (1, 1)):
+                qb(c, i, h)
+
+        def recip(c):
+            rden = accp.tile([P, CH], F32, name="rden", tag="rden")
+            nc.vector.reciprocal(out=rden[:], in_=st[("acc_n_t", c)][:])
+            st[("rden", c)] = rden
+
+        def wgt(c):
+            t1 = accp.tile([P, CH], F32, name="t1", tag="t1")
+            nc.vector.scalar_tensor_tensor(out=t1[:], in0=st[("acc_p_t", c)][:], scalar=0.5,
+                                           in1=st[("rden", c)][:], op0=ALU.mult, op1=ALU.mult)
+            wh = accp.tile([P, CH], F32, name="wh", tag="wh")
+            nc.vector.scalar_tensor_tensor(out=wh[:], in0=bvb[:, c * CH:(c + 1) * CH], scalar=0.5, in1=t1[:],
+                                           op0=ALU.mult, op1=ALU.add)
+            st[("wh", c)] = wh
+
+        def ot(c, pb, tag="ot"):
+            ob = tpools[tag].tile([P, 2, CH], F32, name="ob", tag=tag)
+            for bb in range(2):
+                b = 2 * pb + bb
+                for i in range(2):
+                    nc.tensor.transpose(out=ob[:, bb, i * P:(i + 1) * P],
+                                        in_=st[("th", c, i, b // 4)][:, (b % 4) * P:(b % 4 + 1) * P],
+                                        identity=ident[:])
+            o = outp.tile([P, 2, CH], F32, name="o", tag="o")
+            nc.vector.scalar_tensor_tensor(out=o[:], in0=ob[:], scalar=1.0,
+                                           in1=st[("wh", c)][:].unsqueeze(1).to_broadcast([P, 2, CH]),
+                                           op0=ALU.add, op1=ALU.mult)
+            nc.sync.dma_start(out=out[2 * pb:2 * pb + 2, :, c * CH:(c + 1) * CH].rearrange("b t h -> t b h"),
+                              in_=o[:])
+
+        trx(0, "tr", "V")
+        trx(1, "tr", "S")
+        qx(0)
+        trw("k", 0, 0, "V", "ot")
+        trw("k", 0, 1, "S", "ot")
+        tq("k", 0)
+        trw("v", 0, 0, "V")
+        trw("v", 0, 1, "S")
+        tq("v", 0)
+        trx(2, "ot", "V")
+        trx(3, "ot", "S")
+        qx(1)
+        kb(0, 0)
+        vb(0, 0)
+        trx(4, "tr", "V")
+        trx(5, "tr", "S")
+        qx(2)
+        kb(0, 1)
+        vb(0, 1)
+        trx(6, "ot", "V")
+        trx(7, "ot", "S")
+        qx(3)
+        kb(0, 2)
+        vb(0, 2)
+        trw("q", 0, 0, "V")
+        trw("q", 0, 1, "S")
+        tq("q", 0)
+        bias_stage()
+        kb(0, 3)
+        vb(0, 3)
+        trw("k", 1, 0, "V", "ot")
+        trw("k", 1, 1, "S", "ot")
+        tq("k", 1)
+        trw("v", 1, 0, "V")
+        trw("v", 1, 1)
+        tq("v", 1)
+        q4(0)
+        recip(0)
+        trw("q", 1, 0, "S", "ot")
+        trw("q", 1, 1, "S", "ot")
+        tq("q", 1)
+
+        for c in range(1, NCH):
+            more = c + 1 < NCH
+            kb(c, 0)
+            kb(c, 1)
+            vb(c, 0)
+            kb(c, 2)
+            wgt(c - 1)
+            if more:
+                trw("k", c + 1, 0)
+                trw("k", c + 1, 1)
+            ot(c - 1, 0)
+            ot(c - 1, 1)
+            if more:
+                tq("k", c + 1)
+            kb(c, 3)
+            vb(c, 1)
+            vb(c, 2)
+            vb(c, 3)
+            if more:
+                trw("v", c + 1, 0)
+                trw("v", c + 1, 1)
+            ot(c - 1, 2)
+            ot(c - 1, 3)
+            if more:
+                tq("v", c + 1)
+            q4(c)
+            recip(c)
+            if more:
+                trw("q", c + 1, 0)
+                trw("q", c + 1, 1)
+                tq("q", c + 1)
+        wgt(NCH - 1)
+        ot(NCH - 1, 0)
+        ot(NCH - 1, 1)
+        ot(NCH - 1, 2, "tr")
+        ot(NCH - 1, 3, "tr")

@@ -19,8 +19,8 @@ D = 1024
 H = 1024
 CH = 256
 NCH = H // CH
-PINNED = True
-PSUM_ON_G = True
+NPS = 7
+PREADD = True
 
 
 def tile_aftattention_kernel(tc, x, Wq, bq, Wk, bk, Wv, bv, wbias, out):
@@ -28,30 +28,29 @@ def tile_aftattention_kernel(tc, x, Wq, bq, Wk, bk, Wv, bv, wbias, out):
     with ExitStack() as ctx:
         const = ctx.enter_context(tc.tile_pool(name="const", bufs=1))
         gwp = ctx.enter_context(tc.tile_pool(name="gwp", bufs=4))
-        nump = ctx.enter_context(tc.tile_pool(name="nump", bufs=8))
+        nump = ctx.enter_context(tc.tile_pool(name="nump", bufs=6))
         prodp = ctx.enter_context(tc.tile_pool(name="prodp", bufs=6))
+        addp = ctx.enter_context(tc.tile_pool(name="addp", bufs=3))
         accp = ctx.enter_context(tc.tile_pool(name="accp", bufs=2))
-        thp = ctx.enter_context(tc.tile_pool(name="thp", bufs=12))
+        thp = ctx.enter_context(tc.tile_pool(name="thp", bufs=10))
         outp = ctx.enter_context(tc.tile_pool(name="outp", bufs=4))
-        trp = ctx.enter_context(tc.psum_pool(name="trp", bufs=2))
-        otp = ctx.enter_context(tc.psum_pool(name="otp", bufs=2))
-        mxp = ctx.enter_context(tc.psum_pool(name="mxp", bufs=4))
-        tpools = {"tr": trp, "ot": otp}
-        if PINNED:
-            ctx.enter_context(tc.manual_schedule())
+        psp = ctx.enter_context(tc.psum_pool(name="psp", bufs=NPS))
+        smp = ctx.enter_context(tc.psum_pool(name="smp", bufs=1))
+        ctx.enter_context(tc.manual_schedule())
 
         ident = const.tile([P, P], F32, name="ident")
         make_identity(nc, ident[:])
         identb = const.tile([P, P], BF16, name="identb")
         brow = const.tile([P, P], BF16, name="brow")
-        bvb = const.tile([P, H], BF16, name="bvb")
         warm = const.tile([P, 1], F32, name="warm")
         warm2 = const.tile([P, 1], F32, name="warm2")
         bqh = const.tile([P, 8], F32, name="bqh")
+        bvc = const.tile([P, 8], F32, name="bvc")
         nc.vector.memset(warm[:], 0.0)
         nc.scalar.activation(out=warm2[:], in_=warm[:], func=ACT.Exp)
         nc.vector.memset(brow[:], 0.0)
         nc.scalar.dma_start(out=brow[0:8, :], in_=bq.rearrange("(i p) -> i p", p=P))
+        nc.scalar.dma_start(out=brow[8:16, :], in_=bv.rearrange("(i p) -> i p", p=P))
 
         x_raw = const.tile([P, B * D], BF16, name="x_raw")
         x_raw3 = x_raw[:].rearrange("p (b k) -> p b k", b=B)
@@ -59,49 +58,51 @@ def tile_aftattention_kernel(tc, x, Wq, bq, Wk, bk, Wv, bv, wbias, out):
         w_dram = {"k": Wk, "v": Wv, "q": Wq}
         w_raw = {}
 
-        def load_x(j):
-            nc.sync.dma_start(out=x_raw3[:, 2 * j:2 * j + 2, :], in_=x_t[:, 2 * j:2 * j + 2, :])
+        def load_x(b0, b1):
+            nc.sync.dma_start(out=x_raw3[:, b0:b1, :], in_=x_t[:, b0:b1, :])
 
-        def load_w(w, c):
-            t = const.tile([P, 2 * D], BF16, name="wraw_%s%d" % (w, c))
+        def load_w(w, c, i0, i1):
+            if i0 == 0:
+                t = const.tile([P, 2 * D], BF16, name="wraw_%s%d" % (w, c))
+                w_raw[(w, c)] = t
             nc.sync.dma_start(
-                out=t[:].rearrange("p (i k) -> p i k", i=2),
-                in_=w_dram[w][c * CH:(c + 1) * CH, :].rearrange("(i p) k -> p i k", p=P),
+                out=w_raw[(w, c)][:].rearrange("p (i k) -> p i k", i=2)[:, i0:i1, :],
+                in_=w_dram[w][c * CH + i0 * P:c * CH + i1 * P, :].rearrange("(i p) k -> p i k", p=P),
             )
-            w_raw[(w, c)] = t
 
-        nc.sync.dma_start(out=x_raw3[:, 0:1, :], in_=x_t[:, 0:1, :])
-        nc.sync.dma_start(out=x_raw3[:, 1:2, :], in_=x_t[:, 1:2, :])
-        load_w("k", 0)
-        load_w("v", 0)
-        load_x(1)
-        load_x(2)
-        load_x(3)
-        load_w("q", 0)
+        load_x(0, 1)
+        load_x(1, 2)
+        load_x(2, 4)
+        load_w("k", 0, 0, 1)
+        load_w("k", 0, 1, 2)
+        load_x(4, 6)
+        load_x(6, 8)
+        load_w("v", 0, 0, 2)
+        load_w("q", 0, 0, 2)
         for c in range(1, NCH):
             for w in ("k", "v", "q"):
-                load_w(w, c)
-            if c == 1:
-                nc.sync.dma_start(out=bvb[:], in_=bv.partition_broadcast(P))
+                load_w(w, c, 0, 2)
 
         nc.vector.tensor_copy(out=identb[:], in_=ident[:])
 
         def bias_stage():
-            bt = trp.tile([P, P], BF16, name="bt", tag="tr")
+            bt = psp.tile([P, P], BF16, name="bt", tag="ps")
             nc.tensor.transpose(out=bt[:], in_=brow[:], identity=identb[:])
             nc.vector.tensor_scalar_mul(out=bqh[:], in0=bt[:, 0:8], scalar1=0.5)
+            nc.vector.tensor_copy(out=bvc[:], in_=bt[:, 8:16])
 
         xw = x_raw[:].bitcast(F32)
         gx = [const.tile([P, 2048], F32, name="gx%d" % h, align_bytes=64) for h in range(2)]
         xc = [const.tile([P, 1024], U32, name="xc%d" % h, align_bytes=64) for h in range(2)]
         xs = [const.tile([P, 1024], U8, name="xs%d" % h, align_bytes=64) for h in range(2)]
 
-        def transpose_bank(words, first_col, tag):
-            bank = tpools[tag].tile([P, 4, P], F32, name="trb", tag=tag)
-            for j in range(4):
-                nc.tensor.transpose(out=bank[:, j, :],
-                                    in_=words[:, first_col + 256 * (j // 2) + j % 2:first_col + 256 * (j // 2 + 1):2],
-                                    identity=ident[:])
+        def transpose_bank(words, first_col):
+            bank = psp.tile([P, 4, P], F32, name="trb", tag="ps")
+            for g in range(2):
+                for u in range(2):
+                    lo = first_col + 256 * g
+                    nc.tensor.transpose(out=bank[:, 2 * g + u, :], in_=words[:, lo + u:lo + 256:2],
+                                        identity=ident[:])
             return bank[:].rearrange("p (g u) r -> p g r u", g=2, u=2)
 
         def evac(eng, dst, src):
@@ -110,8 +111,8 @@ def tile_aftattention_kernel(tc, x, Wq, bq, Wk, bk, Wv, bv, wbias, out):
             else:
                 nc.scalar.copy(out=dst, in_=src)
 
-        def trx(b, tag, eng):
-            src = transpose_bank(xw, b * 512, tag)
+        def trx(b, eng):
+            src = transpose_bank(xw, b * 512)
             dst = gx[b // 4][:].rearrange("p (g b r u) -> p g b r u", g=2, b=4, r=P, u=2)[:, :, b % 4, :, :]
             evac(eng, dst, src)
 
@@ -126,11 +127,11 @@ def tile_aftattention_kernel(tc, x, Wq, bq, Wk, bk, Wv, bv, wbias, out):
         ws = {}
         gws = {}
 
-        def trw(w, c, i, eng="S", tag="tr"):
+        def trw(w, c, i, eng="S"):
             if i == 0:
                 gw_new = gwp.tile([P, 1024], F32, name="gw", tag="gw", align_bytes=64)
                 gws[(w, c)] = gw_new
-            src = transpose_bank(w_raw[(w, c)][:].bitcast(F32), i * 512, tag)
+            src = transpose_bank(w_raw[(w, c)][:].bitcast(F32), i * 512)
             dst = gws[(w, c)][:].rearrange("p (g i r u) -> p g i r u", g=2, i=2, r=P, u=2)[:, :, i, :, :]
             evac(eng, dst, src)
 
@@ -142,89 +143,71 @@ def tile_aftattention_kernel(tc, x, Wq, bq, Wk, bk, Wv, bv, wbias, out):
             wc[(w, c)] = codes
             ws[(w, c)] = scales
 
-        def kv_bank(w, c, pb):
-            bank = mxp.tile([P, 2, CH], F32, name="kvb", tag="mx")
-            for bb in range(2):
-                b = 2 * pb + bb
-                h = b // 4
-                for g in range(2):
-                    xcols = slice(g * 512 + (b % 4) * P, g * 512 + (b % 4) * P + P)
-                    wcols = slice(g * CH, (g + 1) * CH)
-                    nc.tensor.matmul_mx(out=bank[:, bb, :],
-                                        lhsT=xc[h][:, xcols].bitcast(FP8X4), lhsT_scale=xs[h][:, xcols],
-                                        rhs=wc[(w, c)][:, wcols].bitcast(FP8X4), rhs_scale=ws[(w, c)][:, wcols],
-                                        start=(g == 0), stop=(g == 1))
-            return bank
-
-        st = {}
-
-        def chain(eng, c, key, tiles, pb):
-            if pb == 1:
-                acc = accp.tile([P, 2, CH], F32, name=key, tag=key)
-                st[(key, c)] = acc
-                eng.tensor_tensor(out=acc[:], in0=tiles[0][:], in1=tiles[1][:], op=ALU.add)
-            elif pb > 1:
-                acc = st[(key, c)]
-                eng.tensor_tensor(out=acc[:], in0=acc[:], in1=tiles[pb][:], op=ALU.add)
-            if pb == 3:
-                acc = st[(key, c)]
-                tot = accp.tile([P, CH], F32, name=key + "_t", tag=key + "_t")
-                eng.tensor_tensor(out=tot[:], in0=acc[:, 0, :], in1=acc[:, 1, :], op=ALU.add)
-                st[(key + "_t", c)] = tot
-
-        def kb(c, pb):
-            bank = kv_bank("k", c, pb)
-            n = nump.tile([P, 2, CH], F32, name="numer", tag="numer")
-            nc.scalar.activation(out=n[:], in_=bank[:], func=ACT.Exp)
-            if pb == 0:
-                st[("numer", c)] = {}
-            st[("numer", c)][pb] = n
-            chain(nc.gpsimd, c, "acc_n", st[("numer", c)], pb)
-
-        def vb(c, pb):
-            bank = kv_bank("v", c, pb)
-            pr = prodp.tile([P, 2, CH], F32, name="prod", tag="prod")
-            nc.vector.tensor_tensor(out=pr[:], in0=bank[:], in1=st[("numer", c)][pb][:], op=ALU.mult)
-            if pb == 0:
-                st[("prod", c)] = {}
-            st[("prod", c)][pb] = pr
-            p_eng = nc.gpsimd if PSUM_ON_G else nc.vector
-            chain(p_eng, c, "acc_p", st[("prod", c)], pb)
-
-        def qb(c, i, h):
-            bank = mxp.tile([P, 512], F32, name="qbank", tag="mx")
+        def mx_bank(w, c, i, h):
+            bank = psp.tile([P, 512], F32, name="mxb", tag="ps")
             for g in range(2):
                 wcols = slice(g * CH + i * P, g * CH + (i + 1) * P)
                 xcols = slice(g * 512, (g + 1) * 512)
                 nc.tensor.matmul_mx(out=bank[:],
-                                    lhsT=wc[("q", c)][:, wcols].bitcast(FP8X4), lhsT_scale=ws[("q", c)][:, wcols],
+                                    lhsT=wc[(w, c)][:, wcols].bitcast(FP8X4), lhsT_scale=ws[(w, c)][:, wcols],
                                     rhs=xc[h][:, xcols].bitcast(FP8X4), rhs_scale=xs[h][:, xcols],
                                     start=(g == 0), stop=(g == 1))
+            return bank
+
+        st = {}
+
+        def pre_add(key, c, i, h, tile):
+            st[(key, c, i, h)] = tile
+            if h == 1 and PREADD and c < NCH - 1:
+                s = addp.tile([P, 512], F32, name="s" + key, tag="s" + key)
+                nc.gpsimd.tensor_tensor(out=s[:], in0=st[(key, c, i, 0)][:], in1=tile[:], op=ALU.add)
+                st[(key, c, i)] = [s]
+            elif h == 1:
+                st[(key, c, i)] = [st[(key, c, i, 0)], tile]
+
+        def kb(c, i, h):
+            bank = mx_bank("k", c, i, h)
+            n = nump.tile([P, 512], F32, name="numer", tag="numer")
+            nc.scalar.activation(out=n[:], in_=bank[:], func=ACT.Exp)
+            pre_add("n", c, i, h, n)
+
+        def vb(c, i, h):
+            bank = mx_bank("v", c, i, h)
+            pr = prodp.tile([P, 512], F32, name="prod", tag="prod")
+            nc.vector.scalar_tensor_tensor(out=pr[:], in0=bank[:], scalar=bvc[:, 2 * c + i:2 * c + i + 1],
+                                           in1=st[("n", c, i, h)][:], op0=ALU.add, op1=ALU.mult)
+            pre_add("p", c, i, h, pr)
+
+        def qb(c, i, h):
+            bank = mx_bank("q", c, i, h)
             t = thp.tile([P, 512], F32, name="th", tag="th")
             nc.scalar.activation(out=t[:], in_=bank[:], func=ACT.Tanh,
                                  bias=bqh[:, 2 * c + i:2 * c + i + 1], scale=0.5)
             st[("th", c, i, h)] = t
 
-        def q4(c):
-            for i, h in ((0, 0), (1, 0), (0, 1), (1, 1)):
-                qb(c, i, h)
+        def batch_sum(key, c, i):
+            if key == "n" and i == 0:
+                sm_new = smp.tile([P, 2, CH], F32, name="sm", tag="sm")
+                st[("sm", c)] = sm_new
+            dst = st[("sm", c)][:, 0 if key == "n" else 1, i * P:(i + 1) * P]
+            parts = [(t, b) for t in st[(key, c, i)] for b in range(4)]
+            for j, (t, b) in enumerate(parts):
+                nc.tensor.matmul(out=dst, lhsT=t[:, b * P:(b + 1) * P], rhs=ident[:], is_transpose=True,
+                                 start=(j == 0), stop=(j == len(parts) - 1))
 
         def recip(c):
             rden = accp.tile([P, CH], F32, name="rden", tag="rden")
-            nc.vector.reciprocal(out=rden[:], in_=st[("acc_n_t", c)][:])
+            nc.vector.reciprocal(out=rden[:], in_=st[("sm", c)][:, 0, :])
             st[("rden", c)] = rden
 
         def wgt(c):
-            t1 = accp.tile([P, CH], F32, name="t1", tag="t1")
-            nc.vector.scalar_tensor_tensor(out=t1[:], in0=st[("acc_p_t", c)][:], scalar=0.5,
-                                           in1=st[("rden", c)][:], op0=ALU.mult, op1=ALU.mult)
             wh = accp.tile([P, CH], F32, name="wh", tag="wh")
-            nc.vector.scalar_tensor_tensor(out=wh[:], in0=bvb[:, c * CH:(c + 1) * CH], scalar=0.5, in1=t1[:],
-                                           op0=ALU.mult, op1=ALU.add)
+            nc.vector.scalar_tensor_tensor(out=wh[:], in0=st[("sm", c)][:, 1, :], scalar=0.5,
+                                           in1=st[("rden", c)][:], op0=ALU.mult, op1=ALU.mult)
             st[("wh", c)] = wh
 
-        def ot(c, pb, tag="ot"):
-            ob = tpools[tag].tile([P, 2, CH], F32, name="ob", tag=tag)
+        def ot(c, pb):
+            ob = psp.tile([P, 2, CH], F32, name="ob", tag="ps")
             for bb in range(2):
                 b = 2 * pb + bb
                 for i in range(2):
@@ -238,81 +221,85 @@ def tile_aftattention_kernel(tc, x, Wq, bq, Wk, bk, Wv, bv, wbias, out):
             nc.sync.dma_start(out=out[2 * pb:2 * pb + 2, :, c * CH:(c + 1) * CH].rearrange("b t h -> t b h"),
                               in_=o[:])
 
-        trx(0, "tr", "V")
-        trx(1, "tr", "S")
+        def four(f, c):
+            for i, h in ((0, 0), (1, 0), (0, 1), (1, 1)):
+                f(c, i, h)
+
+        trx(0, "V")
+        trx(1, "S")
         qx(0)
-        trw("k", 0, 0, "V", "ot")
-        trw("k", 0, 1, "S", "ot")
+        trx(2, "V")
+        trx(3, "S")
+        qx(1)
+        trw("k", 0, 0, "V")
+        trw("k", 0, 1, "S")
         tq("k", 0)
+        trx(4, "V")
+        trx(5, "S")
+        qx(2)
+        kb(0, 0, 0)
+        kb(0, 1, 0)
+        trx(6, "V")
+        trx(7, "S")
+        qx(3)
         trw("v", 0, 0, "V")
         trw("v", 0, 1, "S")
         tq("v", 0)
-        trx(2, "ot", "V")
-        trx(3, "ot", "S")
-        qx(1)
-        kb(0, 0)
-        vb(0, 0)
-        trx(4, "tr", "V")
-        trx(5, "tr", "S")
-        qx(2)
-        kb(0, 1)
-        vb(0, 1)
-        trx(6, "ot", "V")
-        trx(7, "ot", "S")
-        qx(3)
-        kb(0, 2)
-        vb(0, 2)
+        bias_stage()
+        kb(0, 0, 1)
+        kb(0, 1, 1)
         trw("q", 0, 0, "V")
         trw("q", 0, 1, "S")
         tq("q", 0)
-        bias_stage()
-        kb(0, 3)
-        vb(0, 3)
-        trw("k", 1, 0, "V", "ot")
-        trw("k", 1, 1, "S", "ot")
+        four(vb, 0)
+        trw("k", 1, 0, "V")
+        trw("k", 1, 1, "S")
         tq("k", 1)
-        trw("v", 1, 0, "V")
-        trw("v", 1, 1)
-        tq("v", 1)
-        q4(0)
+        batch_sum("n", 0, 0)
+        batch_sum("n", 0, 1)
+        four(qb, 0)
         recip(0)
-        trw("q", 1, 0, "S", "ot")
-        trw("q", 1, 1, "S", "ot")
-        tq("q", 1)
+        trw("v", 1, 0, "V")
+        trw("v", 1, 1, "S")
+        tq("v", 1)
+        batch_sum("p", 0, 0)
+        batch_sum("p", 0, 1)
 
         for c in range(1, NCH):
             more = c + 1 < NCH
-            kb(c, 0)
-            kb(c, 1)
-            vb(c, 0)
-            kb(c, 2)
             wgt(c - 1)
+            four(kb, c)
+            trw("q", c, 0)
+            trw("q", c, 1)
+            ot(c - 1, 0)
+            ot(c - 1, 1)
+            tq("q", c)
+            four(vb, c)
             if more:
                 trw("k", c + 1, 0)
                 trw("k", c + 1, 1)
-            ot(c - 1, 0)
-            ot(c - 1, 1)
+            ot(c - 1, 2)
+            ot(c - 1, 3)
+            batch_sum("n", c, 0)
+            batch_sum("n", c, 1)
             if more:
                 tq("k", c + 1)
-            kb(c, 3)
-            vb(c, 1)
-            vb(c, 2)
-            vb(c, 3)
+            recip(c)
+            qb(c, 0, 0)
+            qb(c, 1, 0)
+            qb(c, 0, 1)
+            if not more:
+                batch_sum("p", c, 0)
+                batch_sum("p", c, 1)
+                wgt(c)
+                ot(c, 0)
+                ot(c, 1)
+            qb(c, 1, 1)
             if more:
                 trw("v", c + 1, 0)
                 trw("v", c + 1, 1)
-            ot(c - 1, 2)
-            ot(c - 1, 3)
-            if more:
                 tq("v", c + 1)
-            q4(c)
-            recip(c)
-            if more:
-                trw("q", c + 1, 0)
-                trw("q", c + 1, 1)
-                tq("q", c + 1)
-        wgt(NCH - 1)
-        ot(NCH - 1, 0)
-        ot(NCH - 1, 1)
-        ot(NCH - 1, 2, "tr")
-        ot(NCH - 1, 3, "tr")
+                batch_sum("p", c, 0)
+                batch_sum("p", c, 1)
+        ot(NCH - 1, 2)
+        ot(NCH - 1, 3)

@@ -34,6 +34,7 @@ def tile_aftattention_kernel(tc, x, Wq, bq, Wk, bk, Wv, bv, wbias, out):
         accp = ctx.enter_context(tc.tile_pool(name="accp", bufs=2))
         thp = ctx.enter_context(tc.tile_pool(name="thp", bufs=10))
         outp = ctx.enter_context(tc.tile_pool(name="outp", bufs=4))
+        wpp = ctx.enter_context(tc.tile_pool(name="wpp", bufs=4))
         psp = ctx.enter_context(tc.psum_pool(name="psp", bufs=NPS))
         smp = ctx.enter_context(tc.psum_pool(name="smp", bufs=1))
         ctx.enter_context(tc.manual_schedule())
@@ -96,13 +97,16 @@ def tile_aftattention_kernel(tc, x, Wq, bq, Wk, bk, Wv, bv, wbias, out):
         xc = [const.tile([P, 1024], U32, name="xc%d" % h, align_bytes=64) for h in range(2)]
         xs = [const.tile([P, 1024], U8, name="xs%d" % h, align_bytes=64) for h in range(2)]
 
-        def transpose_bank(words, first_col):
+        def transpose_bank(words, first_col, sorted_words=False):
             bank = psp.tile([P, 4, P], F32, name="trb", tag="ps")
             for g in range(2):
                 for u in range(2):
                     lo = first_col + 256 * g
-                    nc.tensor.transpose(out=bank[:, 2 * g + u, :], in_=words[:, lo + u:lo + 256:2],
-                                        identity=ident[:])
+                    if sorted_words:
+                        src = words[:, lo + u * P:lo + (u + 1) * P]
+                    else:
+                        src = words[:, lo + u:lo + 256:2]
+                    nc.tensor.transpose(out=bank[:, 2 * g + u, :], in_=src, identity=ident[:])
             return bank[:].rearrange("p (g u) r -> p g r u", g=2, u=2)
 
         def evac(eng, dst, src):
@@ -127,11 +131,22 @@ def tile_aftattention_kernel(tc, x, Wq, bq, Wk, bk, Wv, bv, wbias, out):
         ws = {}
         gws = {}
 
+        w_perm = {}
+
+        def perm(w, c, eng):
+            t = wpp.tile([P, 1024], F32, name="wperm", tag="wperm")
+            evac(eng, t[:].rearrange("p (a u j) -> p a u j", a=4, u=2),
+                 w_raw[(w, c)][:].bitcast(F32).rearrange("p (a j u) -> p a u j", a=4, u=2))
+            w_perm[(w, c)] = t
+
         def trw(w, c, i, eng="S"):
             if i == 0:
                 gw_new = gwp.tile([P, 1024], F32, name="gw", tag="gw", align_bytes=64)
                 gws[(w, c)] = gw_new
-            src = transpose_bank(w_raw[(w, c)][:].bitcast(F32), i * 512)
+            if (w, c) in w_perm:
+                src = transpose_bank(w_perm[(w, c)][:], i * 512, True)
+            else:
+                src = transpose_bank(w_raw[(w, c)][:].bitcast(F32), i * 512)
             dst = gws[(w, c)][:].rearrange("p (g i r u) -> p g i r u", g=2, i=2, r=P, u=2)[:, :, i, :, :]
             evac(eng, dst, src)
 
@@ -186,10 +201,13 @@ def tile_aftattention_kernel(tc, x, Wq, bq, Wk, bk, Wv, bv, wbias, out):
             st[("th", c, i, h)] = t
 
         def batch_sum(key, c, i):
-            if key == "n" and i == 0:
-                sm_new = smp.tile([P, 2, CH], F32, name="sm", tag="sm")
-                st[("sm", c)] = sm_new
-            dst = st[("sm", c)][:, 0 if key == "n" else 1, i * P:(i + 1) * P]
+            if i == 0 and key == "n":
+                den_new = smp.tile([P, CH], F32, name="den", tag="den")
+                st[("sum", "n", c)] = den_new
+            elif i == 0:
+                num_new = psp.tile([P, CH], F32, name="num", tag="ps")
+                st[("sum", "p", c)] = num_new
+            dst = st[("sum", key, c)][:, i * P:(i + 1) * P]
             parts = [(t, b) for t in st[(key, c, i)] for b in range(4)]
             for j, (t, b) in enumerate(parts):
                 nc.tensor.matmul(out=dst, lhsT=t[:, b * P:(b + 1) * P], rhs=ident[:], is_transpose=True,
@@ -197,16 +215,16 @@ def tile_aftattention_kernel(tc, x, Wq, bq, Wk, bk, Wv, bv, wbias, out):
 
         def recip(c):
             rden = accp.tile([P, CH], F32, name="rden", tag="rden")
-            nc.vector.reciprocal(out=rden[:], in_=st[("sm", c)][:, 0, :])
+            nc.vector.reciprocal(out=rden[:], in_=st[("sum", "n", c)][:])
             st[("rden", c)] = rden
 
         def wgt(c):
             wh = accp.tile([P, CH], F32, name="wh", tag="wh")
-            nc.vector.scalar_tensor_tensor(out=wh[:], in0=st[("sm", c)][:, 1, :], scalar=0.5,
+            nc.vector.scalar_tensor_tensor(out=wh[:], in0=st[("sum", "p", c)][:], scalar=0.5,
                                            in1=st[("rden", c)][:], op0=ALU.mult, op1=ALU.mult)
             st[("wh", c)] = wh
 
-        def ot(c, pb):
+        def ot_t(c, pb):
             ob = psp.tile([P, 2, CH], F32, name="ob", tag="ps")
             for bb in range(2):
                 b = 2 * pb + bb
@@ -214,12 +232,20 @@ def tile_aftattention_kernel(tc, x, Wq, bq, Wk, bk, Wv, bv, wbias, out):
                     nc.tensor.transpose(out=ob[:, bb, i * P:(i + 1) * P],
                                         in_=st[("th", c, i, b // 4)][:, (b % 4) * P:(b % 4 + 1) * P],
                                         identity=ident[:])
+            st[("ob", c, pb)] = ob
+
+        def ot_f(c, pb):
+            ob = st[("ob", c, pb)]
             o = outp.tile([P, 2, CH], F32, name="o", tag="o")
             nc.vector.scalar_tensor_tensor(out=o[:], in0=ob[:], scalar=1.0,
                                            in1=st[("wh", c)][:].unsqueeze(1).to_broadcast([P, 2, CH]),
                                            op0=ALU.add, op1=ALU.mult)
             nc.sync.dma_start(out=out[2 * pb:2 * pb + 2, :, c * CH:(c + 1) * CH].rearrange("b t h -> t b h"),
                               in_=o[:])
+
+        def ot(c, pb):
+            ot_t(c, pb)
+            ot_f(c, pb)
 
         def four(f, c):
             for i, h in ((0, 0), (1, 0), (0, 1), (1, 1)):
@@ -228,10 +254,10 @@ def tile_aftattention_kernel(tc, x, Wq, bq, Wk, bk, Wv, bv, wbias, out):
         trx(0, "V")
         trx(1, "S")
         qx(0)
-        trx(2, "V")
-        trx(3, "S")
+        trx(2, "S")
+        trx(3, "V")
         qx(1)
-        trw("k", 0, 0, "V")
+        trw("k", 0, 0, "S")
         trw("k", 0, 1, "S")
         tq("k", 0)
         trx(4, "V")
@@ -251,55 +277,72 @@ def tile_aftattention_kernel(tc, x, Wq, bq, Wk, bk, Wv, bv, wbias, out):
         trw("q", 0, 0, "V")
         trw("q", 0, 1, "S")
         tq("q", 0)
+        perm("k", 1, "S")
         four(vb, 0)
-        trw("k", 1, 0, "V")
+        trw("k", 1, 0, "S")
         trw("k", 1, 1, "S")
         tq("k", 1)
+        perm("v", 1, "V")
         batch_sum("n", 0, 0)
         batch_sum("n", 0, 1)
         four(qb, 0)
         recip(0)
         trw("v", 1, 0, "V")
         trw("v", 1, 1, "S")
+        perm("q", 1, "S")
         tq("v", 1)
         batch_sum("p", 0, 0)
         batch_sum("p", 0, 1)
 
-        for c in range(1, NCH):
-            more = c + 1 < NCH
+        for c in range(1, NCH - 1):
             wgt(c - 1)
+            perm("k", c + 1, "V")
             four(kb, c)
             trw("q", c, 0)
             trw("q", c, 1)
             ot(c - 1, 0)
             ot(c - 1, 1)
             tq("q", c)
+            perm("v", c + 1, "S")
+            perm("q", c + 1, "S")
             four(vb, c)
-            if more:
-                trw("k", c + 1, 0)
-                trw("k", c + 1, 1)
+            trw("k", c + 1, 0)
+            trw("k", c + 1, 1)
             ot(c - 1, 2)
             ot(c - 1, 3)
             batch_sum("n", c, 0)
             batch_sum("n", c, 1)
-            if more:
-                tq("k", c + 1)
+            tq("k", c + 1)
             recip(c)
-            qb(c, 0, 0)
-            qb(c, 1, 0)
-            qb(c, 0, 1)
-            if not more:
-                batch_sum("p", c, 0)
-                batch_sum("p", c, 1)
-                wgt(c)
-                ot(c, 0)
-                ot(c, 1)
-            qb(c, 1, 1)
-            if more:
-                trw("v", c + 1, 0)
-                trw("v", c + 1, 1)
-                tq("v", c + 1)
-                batch_sum("p", c, 0)
-                batch_sum("p", c, 1)
-        ot(NCH - 1, 2)
-        ot(NCH - 1, 3)
+            four(qb, c)
+            trw("v", c + 1, 0)
+            trw("v", c + 1, 1)
+            tq("v", c + 1)
+            batch_sum("p", c, 0)
+            batch_sum("p", c, 1)
+
+        c = NCH - 1
+        wgt(c - 1)
+        four(kb, c)
+        trw("q", c, 0)
+        trw("q", c, 1)
+        ot(c - 1, 0)
+        ot(c - 1, 1)
+        batch_sum("n", c, 0)
+        batch_sum("n", c, 1)
+        tq("q", c)
+        recip(c)
+        four(vb, c)
+        ot_t(c - 1, 2)
+        ot_t(c - 1, 3)
+        qb(c, 0, 0)
+        qb(c, 1, 0)
+        batch_sum("p", c, 0)
+        batch_sum("p", c, 1)
+        qb(c, 0, 1)
+        qb(c, 1, 1)
+        wgt(c)
+        ot_f(c - 1, 2)
+        ot_f(c - 1, 3)
+        for pb in range(4):
+            ot(c, pb)

@@ -20,7 +20,6 @@ H = 1024
 CH = 256
 NCH = H // CH
 NPS = 7
-PREADD = True
 
 
 def tile_aftattention_kernel(tc, x, Wq, bq, Wk, bk, Wv, bv, wbias, out):
@@ -34,6 +33,7 @@ def tile_aftattention_kernel(tc, x, Wq, bq, Wk, bk, Wv, bv, wbias, out):
         accp = ctx.enter_context(tc.tile_pool(name="accp", bufs=2))
         thp = ctx.enter_context(tc.tile_pool(name="thp", bufs=10))
         outp = ctx.enter_context(tc.tile_pool(name="outp", bufs=4))
+        xpp = ctx.enter_context(tc.tile_pool(name="xpp", bufs=4))
         wpp = ctx.enter_context(tc.tile_pool(name="wpp", bufs=4))
         psp = ctx.enter_context(tc.psum_pool(name="psp", bufs=NPS))
         smp = ctx.enter_context(tc.psum_pool(name="smp", bufs=1))
@@ -73,7 +73,8 @@ def tile_aftattention_kernel(tc, x, Wq, bq, Wk, bk, Wv, bv, wbias, out):
 
         load_x(0, 1)
         load_x(1, 2)
-        load_x(2, 4)
+        load_x(2, 3)
+        load_x(3, 4)
         load_w("k", 0, 0, 1)
         load_w("k", 0, 1, 2)
         load_x(4, 6)
@@ -115,8 +116,19 @@ def tile_aftattention_kernel(tc, x, Wq, bq, Wk, bk, Wv, bv, wbias, out):
             else:
                 nc.scalar.copy(out=dst, in_=src)
 
+        x_perm = {}
+
+        def permx(b, eng):
+            t = xpp.tile([P, 512], F32, name="xperm", tag="xperm")
+            evac(eng, t[:].rearrange("p (a u j) -> p a u j", a=2, u=2),
+                 xw[:, b * 512:(b + 1) * 512].rearrange("p (a j u) -> p a u j", a=2, u=2))
+            x_perm[b] = t
+
         def trx(b, eng):
-            src = transpose_bank(xw, b * 512)
+            if b in x_perm:
+                src = transpose_bank(x_perm[b][:], 0, True)
+            else:
+                src = transpose_bank(xw, b * 512)
             dst = gx[b // 4][:].rearrange("p (g b r u) -> p g b r u", g=2, b=4, r=P, u=2)[:, :, b % 4, :, :]
             evac(eng, dst, src)
 
@@ -133,11 +145,12 @@ def tile_aftattention_kernel(tc, x, Wq, bq, Wk, bk, Wv, bv, wbias, out):
 
         w_perm = {}
 
-        def perm(w, c, eng):
-            t = wpp.tile([P, 1024], F32, name="wperm", tag="wperm")
-            evac(eng, t[:].rearrange("p (a u j) -> p a u j", a=4, u=2),
-                 w_raw[(w, c)][:].bitcast(F32).rearrange("p (a j u) -> p a u j", a=4, u=2))
-            w_perm[(w, c)] = t
+        def perm(w, c, eng, i0=0, i1=2):
+            if i0 == 0:
+                wp_new = wpp.tile([P, 1024], F32, name="wperm", tag="wperm")
+                w_perm[(w, c)] = wp_new
+            evac(eng, w_perm[(w, c)][:].rearrange("p (a u j) -> p a u j", a=4, u=2)[:, 2 * i0:2 * i1, :, :],
+                 w_raw[(w, c)][:].bitcast(F32).rearrange("p (a j u) -> p a u j", a=4, u=2)[:, 2 * i0:2 * i1, :, :])
 
         def trw(w, c, i, eng="S"):
             if i == 0:
@@ -173,12 +186,11 @@ def tile_aftattention_kernel(tc, x, Wq, bq, Wk, bk, Wv, bv, wbias, out):
 
         def pre_add(key, c, i, h, tile):
             st[(key, c, i, h)] = tile
-            if h == 1 and PREADD and c < NCH - 1:
+            if h == 1:
                 s = addp.tile([P, 512], F32, name="s" + key, tag="s" + key)
                 nc.gpsimd.tensor_tensor(out=s[:], in0=st[(key, c, i, 0)][:], in1=tile[:], op=ALU.add)
-                st[(key, c, i)] = [s]
-            elif h == 1:
-                st[(key, c, i)] = [st[(key, c, i, 0)], tile]
+                nb = 4
+                st[(key, c, i)] = [(s, b) for b in range(nb)]
 
         def kb(c, i, h):
             bank = mx_bank("k", c, i, h)
@@ -208,21 +220,23 @@ def tile_aftattention_kernel(tc, x, Wq, bq, Wk, bk, Wv, bv, wbias, out):
                 num_new = psp.tile([P, CH], F32, name="num", tag="ps")
                 st[("sum", "p", c)] = num_new
             dst = st[("sum", key, c)][:, i * P:(i + 1) * P]
-            parts = [(t, b) for t in st[(key, c, i)] for b in range(4)]
+            parts = st[(key, c, i)]
             for j, (t, b) in enumerate(parts):
                 nc.tensor.matmul(out=dst, lhsT=t[:, b * P:(b + 1) * P], rhs=ident[:], is_transpose=True,
                                  start=(j == 0), stop=(j == len(parts) - 1))
 
-        def recip(c):
-            rden = accp.tile([P, CH], F32, name="rden", tag="rden")
-            nc.vector.reciprocal(out=rden[:], in_=st[("sum", "n", c)][:])
-            st[("rden", c)] = rden
+        def recip(c, c0=0, c1=CH):
+            if c0 == 0:
+                rden_new = accp.tile([P, CH], F32, name="rden", tag="rden")
+                st[("rden", c)] = rden_new
+            nc.vector.reciprocal(out=st[("rden", c)][:, c0:c1], in_=st[("sum", "n", c)][:, c0:c1])
 
-        def wgt(c):
-            wh = accp.tile([P, CH], F32, name="wh", tag="wh")
-            nc.vector.scalar_tensor_tensor(out=wh[:], in0=st[("sum", "p", c)][:], scalar=0.5,
-                                           in1=st[("rden", c)][:], op0=ALU.mult, op1=ALU.mult)
-            st[("wh", c)] = wh
+        def wgt(c, c0=0, c1=CH):
+            if c0 == 0:
+                wh_new = accp.tile([P, CH], F32, name="wh", tag="wh")
+                st[("wh", c)] = wh_new
+            nc.vector.scalar_tensor_tensor(out=st[("wh", c)][:, c0:c1], in0=st[("sum", "p", c)][:, c0:c1], scalar=0.5,
+                                           in1=st[("rden", c)][:, c0:c1], op0=ALU.mult, op1=ALU.mult)
 
         def ot_t(c, pb):
             ob = psp.tile([P, 2, CH], F32, name="ob", tag="ps")
@@ -247,57 +261,88 @@ def tile_aftattention_kernel(tc, x, Wq, bq, Wk, bk, Wv, bv, wbias, out):
             ot_t(c, pb)
             ot_f(c, pb)
 
-        def four(f, c):
-            for i, h in ((0, 0), (1, 0), (0, 1), (1, 1)):
-                f(c, i, h)
+        def oti_t(c, i, h):
+            ob = psp.tile([P, 4, P], F32, name="obi", tag="ps")
+            for b in range(4):
+                nc.tensor.transpose(out=ob[:, b, :], in_=st[("th", c, i, h)][:, b * P:(b + 1) * P], identity=ident[:])
+            st[("obi", c, i, h)] = ob
 
-        trx(0, "V")
+        def oti_f(c, i, h):
+            o = outp.tile([P, 4, P], F32, name="oi", tag="o")
+            nc.vector.scalar_tensor_tensor(
+                out=o[:], in0=st[("obi", c, i, h)][:], scalar=1.0,
+                in1=st[("wh", c)][:, i * P:(i + 1) * P].unsqueeze(1).to_broadcast([P, 4, P]),
+                op0=ALU.add, op1=ALU.mult)
+            h0 = c * CH + i * P
+            nc.sync.dma_start(out=out[4 * h:4 * h + 4, :, h0:h0 + P].rearrange("b t h -> t b h"), in_=o[:])
+
+        def two(f, c, i):
+            f(c, i, 0)
+            f(c, i, 1)
+
+        def four(f, c):
+            two(f, c, 0)
+            two(f, c, 1)
+
+        permx(0, "V")
+        trx(0, "S")
+        permx(1, "V")
         trx(1, "S")
-        qx(0)
+        permx(2, "V")
         trx(2, "S")
-        trx(3, "V")
-        qx(1)
+        permx(3, "V")
+        trx(3, "S")
+        perm("k", 0, "V", 0, 1)
         trw("k", 0, 0, "S")
+        qx(0)
+        perm("k", 0, "V", 1, 2)
         trw("k", 0, 1, "S")
+        qx(1)
+        permx(4, "V")
+        permx(5, "V")
+        trx(4, "S")
         tq("k", 0)
-        trx(4, "V")
+        permx(6, "V")
+        permx(7, "V")
         trx(5, "S")
-        qx(2)
         kb(0, 0, 0)
         kb(0, 1, 0)
+        perm("v", 0, "V")
+        perm("q", 0, "V")
         trx(6, "V")
         trx(7, "S")
-        qx(3)
+        qx(2)
         trw("v", 0, 0, "V")
         trw("v", 0, 1, "S")
-        tq("v", 0)
         bias_stage()
-        kb(0, 0, 1)
-        kb(0, 1, 1)
+        qx(3)
+        tq("v", 0)
         trw("q", 0, 0, "V")
         trw("q", 0, 1, "S")
-        tq("q", 0)
         perm("k", 1, "S")
+        kb(0, 0, 1)
+        kb(0, 1, 1)
+        tq("q", 0)
         four(vb, 0)
         trw("k", 1, 0, "S")
         trw("k", 1, 1, "S")
+        perm("v", 1, "S")
         tq("k", 1)
-        perm("v", 1, "V")
+        four(qb, 0)
         batch_sum("n", 0, 0)
         batch_sum("n", 0, 1)
-        four(qb, 0)
-        recip(0)
-        trw("v", 1, 0, "V")
+        trw("v", 1, 0, "S")
         trw("v", 1, 1, "S")
         perm("q", 1, "S")
+        recip(0)
         tq("v", 1)
-        batch_sum("p", 0, 0)
-        batch_sum("p", 0, 1)
 
         for c in range(1, NCH - 1):
-            wgt(c - 1)
             perm("k", c + 1, "V")
             four(kb, c)
+            batch_sum("p", c - 1, 0)
+            batch_sum("p", c - 1, 1)
+            wgt(c - 1)
             trw("q", c, 0)
             trw("q", c, 1)
             ot(c - 1, 0)
@@ -318,31 +363,29 @@ def tile_aftattention_kernel(tc, x, Wq, bq, Wk, bk, Wv, bv, wbias, out):
             trw("v", c + 1, 0)
             trw("v", c + 1, 1)
             tq("v", c + 1)
-            batch_sum("p", c, 0)
-            batch_sum("p", c, 1)
 
         c = NCH - 1
-        wgt(c - 1)
         four(kb, c)
+        batch_sum("p", c - 1, 0)
+        batch_sum("p", c - 1, 1)
+        wgt(c - 1)
         trw("q", c, 0)
         trw("q", c, 1)
         ot(c - 1, 0)
         ot(c - 1, 1)
+        tq("q", c)
+        four(vb, c)
+        ot(c - 1, 2)
+        ot(c - 1, 3)
         batch_sum("n", c, 0)
         batch_sum("n", c, 1)
-        tq("q", c)
         recip(c)
-        four(vb, c)
-        ot_t(c - 1, 2)
-        ot_t(c - 1, 3)
-        qb(c, 0, 0)
-        qb(c, 1, 0)
+        four(qb, c)
         batch_sum("p", c, 0)
+        wgt(c, 0, P)
+        two(oti_t, c, 0)
+        two(oti_f, c, 0)
         batch_sum("p", c, 1)
-        qb(c, 0, 1)
-        qb(c, 1, 1)
-        wgt(c)
-        ot_f(c - 1, 2)
-        ot_f(c - 1, 3)
-        for pb in range(4):
-            ot(c, pb)
+        wgt(c, P, CH)
+        two(oti_t, c, 1)
+        two(oti_f, c, 1)

@@ -27,14 +27,15 @@ def tile_aftattention_kernel(tc, x, Wq, bq, Wk, bk, Wv, bv, wbias, out):
     with ExitStack() as ctx:
         const = ctx.enter_context(tc.tile_pool(name="const", bufs=1))
         gwp = ctx.enter_context(tc.tile_pool(name="gwp", bufs=4))
-        nump = ctx.enter_context(tc.tile_pool(name="nump", bufs=6))
+        nump = ctx.enter_context(tc.tile_pool(name="nump", bufs=8))
         prodp = ctx.enter_context(tc.tile_pool(name="prodp", bufs=6))
         addp = ctx.enter_context(tc.tile_pool(name="addp", bufs=3))
         accp = ctx.enter_context(tc.tile_pool(name="accp", bufs=2))
         thp = ctx.enter_context(tc.tile_pool(name="thp", bufs=10))
         outp = ctx.enter_context(tc.tile_pool(name="outp", bufs=4))
         xpp = ctx.enter_context(tc.tile_pool(name="xpp", bufs=4))
-        wpp = ctx.enter_context(tc.tile_pool(name="wpp", bufs=4))
+        wrp = ctx.enter_context(tc.tile_pool(name="wrp", bufs=8))
+        wpp = ctx.enter_context(tc.tile_pool(name="wpp", bufs=6))
         psp = ctx.enter_context(tc.psum_pool(name="psp", bufs=NPS))
         smp = ctx.enter_context(tc.psum_pool(name="smp", bufs=1))
         ctx.enter_context(tc.manual_schedule())
@@ -64,7 +65,7 @@ def tile_aftattention_kernel(tc, x, Wq, bq, Wk, bk, Wv, bv, wbias, out):
 
         def load_w(w, c, i0, i1):
             if i0 == 0:
-                t = const.tile([P, 2 * D], BF16, name="wraw_%s%d" % (w, c))
+                t = wrp.tile([P, 2 * D], BF16, name="wraw", tag="wraw")
                 w_raw[(w, c)] = t
             nc.sync.dma_start(
                 out=w_raw[(w, c)][:].rearrange("p (i k) -> p i k", i=2)[:, i0:i1, :],
@@ -77,8 +78,8 @@ def tile_aftattention_kernel(tc, x, Wq, bq, Wk, bk, Wv, bv, wbias, out):
         load_x(3, 4)
         load_w("k", 0, 0, 1)
         load_w("k", 0, 1, 2)
-        load_x(4, 6)
-        load_x(6, 8)
+        for b in range(4, 8):
+            load_x(b, b + 1)
         load_w("v", 0, 0, 2)
         load_w("q", 0, 0, 2)
         for c in range(1, NCH):
@@ -113,6 +114,8 @@ def tile_aftattention_kernel(tc, x, Wq, bq, Wk, bk, Wv, bv, wbias, out):
         def evac(eng, dst, src):
             if eng == "V":
                 nc.vector.tensor_copy(out=dst, in_=src)
+            elif eng == "G":
+                nc.gpsimd.tensor_copy(out=dst, in_=src)
             else:
                 nc.scalar.copy(out=dst, in_=src)
 
@@ -190,6 +193,11 @@ def tile_aftattention_kernel(tc, x, Wq, bq, Wk, bk, Wv, bv, wbias, out):
                 s = addp.tile([P, 512], F32, name="s" + key, tag="s" + key)
                 nc.gpsimd.tensor_tensor(out=s[:], in0=st[(key, c, i, 0)][:], in1=tile[:], op=ALU.add)
                 nb = 4
+                if 0 < c < NCH - 1:
+                    s2 = addp.tile([P, 256], F32, name="r" + key, tag="r" + key)
+                    nc.gpsimd.tensor_tensor(out=s2[:], in0=s[:, 0:256], in1=s[:, 256:512], op=ALU.add)
+                    s = s2
+                    nb = 2
                 st[(key, c, i)] = [(s, b) for b in range(nb)]
 
         def kb(c, i, h):
@@ -294,93 +302,94 @@ def tile_aftattention_kernel(tc, x, Wq, bq, Wk, bk, Wv, bv, wbias, out):
         trx(3, "S")
         perm("k", 0, "V", 0, 1)
         trw("k", 0, 0, "S")
-        qx(0)
         perm("k", 0, "V", 1, 2)
+        qx(0)
         trw("k", 0, 1, "S")
-        qx(1)
         permx(4, "V")
-        permx(5, "V")
         trx(4, "S")
+        qx(1)
+        permx(5, "V")
+        trx(5, "S")
         tq("k", 0)
         permx(6, "V")
         permx(7, "V")
-        trx(5, "S")
         kb(0, 0, 0)
         kb(0, 1, 0)
+        qx(2)
         perm("v", 0, "V")
-        perm("q", 0, "V")
         trx(6, "V")
         trx(7, "S")
-        qx(2)
+        perm("q", 0, "V")
+        qx(3)
         trw("v", 0, 0, "V")
         trw("v", 0, 1, "S")
         bias_stage()
-        qx(3)
         tq("v", 0)
         trw("q", 0, 0, "V")
         trw("q", 0, 1, "S")
-        perm("k", 1, "S")
+        perm("k", 1, "G")
+        perm("v", 1, "G")
+        perm("q", 1, "G")
         kb(0, 0, 1)
         kb(0, 1, 1)
         tq("q", 0)
         four(vb, 0)
         trw("k", 1, 0, "S")
         trw("k", 1, 1, "S")
-        perm("v", 1, "S")
-        tq("k", 1)
-        four(qb, 0)
-        batch_sum("n", 0, 0)
-        batch_sum("n", 0, 1)
         trw("v", 1, 0, "S")
         trw("v", 1, 1, "S")
-        perm("q", 1, "S")
-        recip(0)
+        tq("k", 1)
         tq("v", 1)
+        batch_sum("n", 0, 0)
+        batch_sum("n", 0, 1)
+        recip(0)
+        perm("k", 2, "G")
 
         for c in range(1, NCH - 1):
-            perm("k", c + 1, "V")
+            four(qb, c - 1)
             four(kb, c)
+            trw("q", c, 0)
+            trw("q", c, 1)
             batch_sum("p", c - 1, 0)
             batch_sum("p", c - 1, 1)
             wgt(c - 1)
-            trw("q", c, 0)
-            trw("q", c, 1)
-            ot(c - 1, 0)
-            ot(c - 1, 1)
+            for pb in range(4):
+                ot(c - 1, pb)
             tq("q", c)
-            perm("v", c + 1, "S")
-            perm("q", c + 1, "S")
+            if c == 1:
+                perm("v", 2, "G")
+            perm("q", c + 1, "G")
+            if c + 2 < NCH:
+                perm("k", c + 2, "S")
+                perm("v", c + 2, "S")
             four(vb, c)
             trw("k", c + 1, 0)
             trw("k", c + 1, 1)
-            ot(c - 1, 2)
-            ot(c - 1, 3)
+            trw("v", c + 1, 0)
+            trw("v", c + 1, 1, "V")
             batch_sum("n", c, 0)
             batch_sum("n", c, 1)
             tq("k", c + 1)
-            recip(c)
-            four(qb, c)
-            trw("v", c + 1, 0)
-            trw("v", c + 1, 1)
             tq("v", c + 1)
+            recip(c)
 
         c = NCH - 1
+        four(qb, c - 1)
         four(kb, c)
+        trw("q", c, 0)
+        trw("q", c, 1)
         batch_sum("p", c - 1, 0)
         batch_sum("p", c - 1, 1)
         wgt(c - 1)
-        trw("q", c, 0)
-        trw("q", c, 1)
-        ot(c - 1, 0)
-        ot(c - 1, 1)
+        for pb in range(4):
+            ot(c - 1, pb)
         tq("q", c)
         four(vb, c)
-        ot(c - 1, 2)
-        ot(c - 1, 3)
         batch_sum("n", c, 0)
         batch_sum("n", c, 1)
         recip(c)
-        four(qb, c)
+        two(qb, c, 0)
+        two(qb, c, 1)
         batch_sum("p", c, 0)
         wgt(c, 0, P)
         two(oti_t, c, 0)

@@ -327,9 +327,7 @@ def tile_aftattention_kernel(tc, x, Wq, bq, Wk, bk, Wv, bv, wbias, out):
         tq("v", 0)
         trw("q", 0, 0, "V")
         trw("q", 0, 1, "S")
-        perm("k", 1, "G")
-        perm("v", 1, "G")
-        perm("q", 1, "G")
+        perm("k", 1, "S")
         kb(0, 0, 1)
         kb(0, 1, 1)
         tq("q", 0)
@@ -343,7 +341,8 @@ def tile_aftattention_kernel(tc, x, Wq, bq, Wk, bk, Wv, bv, wbias, out):
         batch_sum("n", 0, 0)
         batch_sum("n", 0, 1)
         recip(0)
-        perm("k", 2, "G")
+        perm("q", 1, "V")
+        perm("k", 2, "S")
 
         for c in range(1, NCH - 1):
             four(qb, c - 1)
@@ -357,8 +356,8 @@ def tile_aftattention_kernel(tc, x, Wq, bq, Wk, bk, Wv, bv, wbias, out):
                 ot(c - 1, pb)
             tq("q", c)
             if c == 1:
-                perm("v", 2, "G")
-            perm("q", c + 1, "G")
+                perm("v", 2, "S")
+            perm("q", c + 1, "S")
             if c + 2 < NCH:
                 perm("k", c + 2, "S")
                 perm("v", c + 2, "S")
@@ -366,7 +365,7 @@ def tile_aftattention_kernel(tc, x, Wq, bq, Wk, bk, Wv, bv, wbias, out):
             trw("k", c + 1, 0)
             trw("k", c + 1, 1)
             trw("v", c + 1, 0)
-            trw("v", c + 1, 1, "V")
+            trw("v", c + 1, 1)
             batch_sum("n", c, 0)
             batch_sum("n", c, 1)
             tq("k", c + 1)

@@ -50,6 +50,8 @@ def tile_aftattention_kernel(tc, x, Wq, bq, Wk, bk, Wv, bv, wbias, out):
         bvc = const.tile([P, 8], F32, name="bvc")
         nc.vector.memset(warm[:], 0.0)
         nc.scalar.activation(out=warm2[:], in_=warm[:], func=ACT.Exp)
+        zeros = const.tile([P, 512], BF16, name="zeros")
+        nc.vector.memset(zeros[:], 0.0)
         nc.vector.memset(brow[:], 0.0)
         nc.scalar.dma_start(out=brow[0:8, :], in_=bq.rearrange("(i p) -> i p", p=P))
         nc.scalar.dma_start(out=brow[8:16, :], in_=bv.rearrange("(i p) -> i p", p=P))
@@ -146,6 +148,12 @@ def tile_aftattention_kernel(tc, x, Wq, bq, Wk, bk, Wv, bv, wbias, out):
         ws = {}
         gws = {}
 
+        idle_bank = smp.tile([P, 512], F32, name="idle_bank", tag="den")
+
+        def keep_warm(n, cols=512):
+            for j in range(n):
+                nc.tensor.matmul(out=idle_bank[:, 0:cols], lhsT=zeros[:, 0:P], rhs=zeros[:, 0:cols], start=True, stop=True)
+
         w_perm = {}
 
         def perm(w, c, eng, i0=0, i1=2):
@@ -222,7 +230,7 @@ def tile_aftattention_kernel(tc, x, Wq, bq, Wk, bk, Wv, bv, wbias, out):
 
         def batch_sum(key, c, i):
             if i == 0 and key == "n":
-                den_new = smp.tile([P, CH], F32, name="den", tag="den")
+                den_new = smp.tile([P, 512], F32, name="den", tag="den")
                 st[("sum", "n", c)] = den_new
             elif i == 0:
                 num_new = psp.tile([P, CH], F32, name="num", tag="ps")
@@ -292,6 +300,7 @@ def tile_aftattention_kernel(tc, x, Wq, bq, Wk, bk, Wv, bv, wbias, out):
             two(f, c, 0)
             two(f, c, 1)
 
+        keep_warm(5)
         permx(0, "V")
         trx(0, "S")
         permx(1, "V")
@@ -332,6 +341,7 @@ def tile_aftattention_kernel(tc, x, Wq, bq, Wk, bk, Wv, bv, wbias, out):
         kb(0, 1, 1)
         tq("q", 0)
         four(vb, 0)
+        perm("q", 1, "V")
         trw("k", 1, 0, "S")
         trw("k", 1, 1, "S")
         trw("v", 1, 0, "S")
@@ -341,17 +351,16 @@ def tile_aftattention_kernel(tc, x, Wq, bq, Wk, bk, Wv, bv, wbias, out):
         batch_sum("n", 0, 0)
         batch_sum("n", 0, 1)
         recip(0)
-        perm("q", 1, "V")
         perm("k", 2, "S")
 
         for c in range(1, NCH - 1):
             four(qb, c - 1)
             four(kb, c)
-            trw("q", c, 0)
-            trw("q", c, 1)
             batch_sum("p", c - 1, 0)
             batch_sum("p", c - 1, 1)
             wgt(c - 1)
+            trw("q", c, 0)
+            trw("q", c, 1)
             for pb in range(4):
                 ot(c - 1, pb)
             tq("q", c)
@@ -375,11 +384,11 @@ def tile_aftattention_kernel(tc, x, Wq, bq, Wk, bk, Wv, bv, wbias, out):
         c = NCH - 1
         four(qb, c - 1)
         four(kb, c)
-        trw("q", c, 0)
-        trw("q", c, 1)
         batch_sum("p", c - 1, 0)
         batch_sum("p", c - 1, 1)
         wgt(c - 1)
+        trw("q", c, 0)
+        trw("q", c, 1)
         for pb in range(4):
             ot(c - 1, pb)
         tq("q", c)

@@ -50,8 +50,6 @@ def tile_aftattention_kernel(tc, x, Wq, bq, Wk, bk, Wv, bv, wbias, out):
         bvc = const.tile([P, 8], F32, name="bvc")
         nc.vector.memset(warm[:], 0.0)
         nc.scalar.activation(out=warm2[:], in_=warm[:], func=ACT.Exp)
-        zeros = const.tile([P, 512], BF16, name="zeros")
-        nc.vector.memset(zeros[:], 0.0)
         nc.vector.memset(brow[:], 0.0)
         nc.scalar.dma_start(out=brow[0:8, :], in_=bq.rearrange("(i p) -> i p", p=P))
         nc.scalar.dma_start(out=brow[8:16, :], in_=bv.rearrange("(i p) -> i p", p=P))
@@ -148,12 +146,6 @@ def tile_aftattention_kernel(tc, x, Wq, bq, Wk, bk, Wv, bv, wbias, out):
         ws = {}
         gws = {}
 
-        idle_bank = smp.tile([P, 512], F32, name="idle_bank", tag="den")
-
-        def keep_warm(n, cols=512):
-            for j in range(n):
-                nc.tensor.matmul(out=idle_bank[:, 0:cols], lhsT=zeros[:, 0:P], rhs=zeros[:, 0:cols], start=True, stop=True)
-
         w_perm = {}
 
         def perm(w, c, eng, i0=0, i1=2):
@@ -201,7 +193,7 @@ def tile_aftattention_kernel(tc, x, Wq, bq, Wk, bk, Wv, bv, wbias, out):
                 s = addp.tile([P, 512], F32, name="s" + key, tag="s" + key)
                 nc.gpsimd.tensor_tensor(out=s[:], in0=st[(key, c, i, 0)][:], in1=tile[:], op=ALU.add)
                 nb = 4
-                if 0 < c < NCH - 1:
+                if key == "p" and 0 < c < NCH - 1:
                     s2 = addp.tile([P, 256], F32, name="r" + key, tag="r" + key)
                     nc.gpsimd.tensor_tensor(out=s2[:], in0=s[:, 0:256], in1=s[:, 256:512], op=ALU.add)
                     s = s2
@@ -230,7 +222,7 @@ def tile_aftattention_kernel(tc, x, Wq, bq, Wk, bk, Wv, bv, wbias, out):
 
         def batch_sum(key, c, i):
             if i == 0 and key == "n":
-                den_new = smp.tile([P, 512], F32, name="den", tag="den")
+                den_new = smp.tile([P, CH], F32, name="den", tag="den")
                 st[("sum", "n", c)] = den_new
             elif i == 0:
                 num_new = psp.tile([P, CH], F32, name="num", tag="ps")
@@ -300,7 +292,6 @@ def tile_aftattention_kernel(tc, x, Wq, bq, Wk, bk, Wv, bv, wbias, out):
             two(f, c, 0)
             two(f, c, 1)
 
-        keep_warm(5)
         permx(0, "V")
         trx(0, "S")
         permx(1, "V")
@@ -330,7 +321,7 @@ def tile_aftattention_kernel(tc, x, Wq, bq, Wk, bk, Wv, bv, wbias, out):
         trx(7, "S")
         perm("q", 0, "V")
         qx(3)
-        trw("v", 0, 0, "V")
+        trw("v", 0, 0, "S")
         trw("v", 0, 1, "S")
         bias_stage()
         tq("v", 0)
@@ -342,7 +333,7 @@ def tile_aftattention_kernel(tc, x, Wq, bq, Wk, bk, Wv, bv, wbias, out):
         tq("q", 0)
         four(vb, 0)
         perm("q", 1, "V")
-        trw("k", 1, 0, "S")
+        trw("k", 1, 0, "V")
         trw("k", 1, 1, "S")
         trw("v", 1, 0, "S")
         trw("v", 1, 1, "S")
@@ -380,6 +371,10 @@ def tile_aftattention_kernel(tc, x, Wq, bq, Wk, bk, Wv, bv, wbias, out):
             tq("k", c + 1)
             tq("v", c + 1)
             recip(c)
+            if c == NCH - 2:
+                trw("q", c + 1, 0)
+                trw("q", c + 1, 1)
+                tq("q", c + 1)
 
         c = NCH - 1
         four(qb, c - 1)
@@ -387,11 +382,8 @@ def tile_aftattention_kernel(tc, x, Wq, bq, Wk, bk, Wv, bv, wbias, out):
         batch_sum("p", c - 1, 0)
         batch_sum("p", c - 1, 1)
         wgt(c - 1)
-        trw("q", c, 0)
-        trw("q", c, 1)
         for pb in range(4):
             ot(c - 1, pb)
-        tq("q", c)
         four(vb, c)
         batch_sum("n", c, 0)
         batch_sum("n", c, 1)

@@ -33,7 +33,6 @@ def tile_aftattention_kernel(tc, x, Wq, bq, Wk, bk, Wv, bv, wbias, out):
         accp = ctx.enter_context(tc.tile_pool(name="accp", bufs=2))
         thp = ctx.enter_context(tc.tile_pool(name="thp", bufs=10))
         outp = ctx.enter_context(tc.tile_pool(name="outp", bufs=4))
-        xpp = ctx.enter_context(tc.tile_pool(name="xpp", bufs=4))
         wrp = ctx.enter_context(tc.tile_pool(name="wrp", bufs=8))
         wpp = ctx.enter_context(tc.tile_pool(name="wpp", bufs=6))
         psp = ctx.enter_context(tc.psum_pool(name="psp", bufs=NPS))
@@ -119,19 +118,8 @@ def tile_aftattention_kernel(tc, x, Wq, bq, Wk, bk, Wv, bv, wbias, out):
             else:
                 nc.scalar.copy(out=dst, in_=src)
 
-        x_perm = {}
-
-        def permx(b, eng):
-            t = xpp.tile([P, 512], F32, name="xperm", tag="xperm")
-            evac(eng, t[:].rearrange("p (a u j) -> p a u j", a=2, u=2),
-                 xw[:, b * 512:(b + 1) * 512].rearrange("p (a j u) -> p a u j", a=2, u=2))
-            x_perm[b] = t
-
         def trx(b, eng):
-            if b in x_perm:
-                src = transpose_bank(x_perm[b][:], 0, True)
-            else:
-                src = transpose_bank(xw, b * 512)
+            src = transpose_bank(xw, b * 512)
             dst = gx[b // 4][:].rearrange("p (g b r u) -> p g b r u", g=2, b=4, r=P, u=2)[:, :, b % 4, :, :]
             evac(eng, dst, src)
 
@@ -292,27 +280,17 @@ def tile_aftattention_kernel(tc, x, Wq, bq, Wk, bk, Wv, bv, wbias, out):
             two(f, c, 0)
             two(f, c, 1)
 
-        permx(0, "V")
         trx(0, "S")
-        permx(1, "V")
         trx(1, "S")
-        permx(2, "V")
         trx(2, "S")
-        permx(3, "V")
         trx(3, "S")
-        perm("k", 0, "V", 0, 1)
         trw("k", 0, 0, "S")
-        perm("k", 0, "V", 1, 2)
         qx(0)
         trw("k", 0, 1, "S")
-        permx(4, "V")
         trx(4, "S")
         qx(1)
-        permx(5, "V")
         trx(5, "S")
         tq("k", 0)
-        permx(6, "V")
-        permx(7, "V")
         kb(0, 0, 0)
         kb(0, 1, 0)
         qx(2)

@@ -333,12 +333,10 @@ def tile_aftattention_kernel(tc, x, Wq, bq, Wk, bk, Wv, bv, wbias, out):
             for pb in range(4):
                 ot(c - 1, pb)
             tq("q", c)
-            if c == 1:
-                perm("v", 2, "S")
+            perm("v", c + 1, "S")
             perm("q", c + 1, "S")
             if c + 2 < NCH:
                 perm("k", c + 2, "S")
-                perm("v", c + 2, "S")
             four(vb, c)
             trw("k", c + 1, 0)
             trw("k", c + 1, 1)

@@ -95,8 +95,8 @@ def tile_aftattention_kernel(tc, x, Wq, bq, Wk, bk, Wv, bv, wbias, out):
 
         xw = x_raw[:].bitcast(F32)
         gx = [const.tile([P, 2048], F32, name="gx%d" % h, align_bytes=64) for h in range(2)]
-        xc = [const.tile([P, 1024], U32, name="xc%d" % h, align_bytes=64) for h in range(2)]
-        xs = [const.tile([P, 1024], U8, name="xs%d" % h, align_bytes=64) for h in range(2)]
+        xc = [const.tile([P, 1024], U32, name="xc%d" % h, align_bytes=256) for h in range(2)]
+        xs = [const.tile([P, 1024], U8, name="xs%d" % h, align_bytes=256) for h in range(2)]
 
         def transpose_bank(words, first_col, sorted_words=False):
             bank = psp.tile([P, 4, P], F32, name="trb", tag="ps")
@@ -155,10 +155,11 @@ def tile_aftattention_kernel(tc, x, Wq, bq, Wk, bk, Wv, bv, wbias, out):
             evac(eng, dst, src)
 
         def tq(w, c):
-            codes = const.tile([P, 512], U32, name="wc_%s%d" % (w, c), align_bytes=64)
-            scales = const.tile([P, 512], U8, name="ws_%s%d" % (w, c), align_bytes=64)
-            nc.vector.quantize_mx(out=codes[:].bitcast(FP8X4), scales=scales[:],
-                                  in_=gws[(w, c)][:].bitcast(BF16))
+            codes_all = const.tile([P, 544], U32, name="wc_%s%d" % (w, c), align_bytes=256)
+            scales_all = const.tile([P, 576], U8, name="ws_%s%d" % (w, c), align_bytes=256)
+            codes = codes_all[:, 32:544]
+            scales = scales_all[:, 64:576]
+            nc.vector.quantize_mx(out=codes.bitcast(FP8X4), scales=scales, in_=gws[(w, c)][:].bitcast(BF16))
             wc[(w, c)] = codes
             ws[(w, c)] = scales
 

@@ -47,6 +47,14 @@ def tile_aftattention_kernel(tc, x, Wq, bq, Wk, bk, Wv, bv, wbias, out):
         warm2 = const.tile([P, 1], F32, name="warm2")
         bqh = const.tile([P, 8], F32, name="bqh")
         bvc = const.tile([P, 8], F32, name="bvc")
+        zt = const.tile([P, 512], BF16, name="zt")
+        nc.vector.memset(zt[:], 0.0)
+
+        def dummy(n):
+            bank = psp.tile([P, 512], F32, name="dm", tag="ps")
+            for r in range(n):
+                nc.tensor.matmul(out=bank[:], lhsT=zt[:, 0:P], rhs=zt[:], start=True, stop=True)
+
         nc.vector.memset(warm[:], 0.0)
         nc.scalar.activation(out=warm2[:], in_=warm[:], func=ACT.Exp)
         nc.vector.memset(brow[:], 0.0)
@@ -292,6 +300,7 @@ def tile_aftattention_kernel(tc, x, Wq, bq, Wk, bk, Wv, bv, wbias, out):
         qx(1)
         trx(5, "S")
         tq("k", 0)
+        dummy(2)
         kb(0, 0, 0)
         kb(0, 1, 0)
         qx(2)
@@ -304,6 +313,7 @@ def tile_aftattention_kernel(tc, x, Wq, bq, Wk, bk, Wv, bv, wbias, out):
         trw("v", 0, 1, "S")
         bias_stage()
         tq("v", 0)
+        dummy(2)
         trw("q", 0, 0, "V")
         trw("q", 0, 1, "S")
         perm("k", 1, "S")

@@ -184,18 +184,20 @@ def tile_aftattention_kernel(tc, x, Wq, bq, Wk, bk, Wv, bv, wbias, out):
 
         st = {}
 
+        def second_add(key, c, i, eng):
+            s = st[(key, c, i)][0][0]
+            s2 = addp.tile([P, 256], F32, name="r" + key, tag="r" + key)
+            eng.tensor_tensor(out=s2[:], in0=s[:, 0:256], in1=s[:, 256:512], op=ALU.add)
+            st[(key, c, i)] = [(s2, 0), (s2, 1)]
+
         def pre_add(key, c, i, h, tile):
             st[(key, c, i, h)] = tile
             if h == 1:
                 s = addp.tile([P, 512], F32, name="s" + key, tag="s" + key)
                 nc.gpsimd.tensor_tensor(out=s[:], in0=st[(key, c, i, 0)][:], in1=tile[:], op=ALU.add)
-                nb = 4
-                if key == "p" and 0 < c < NCH - 1:
-                    s2 = addp.tile([P, 256], F32, name="r" + key, tag="r" + key)
-                    nc.gpsimd.tensor_tensor(out=s2[:], in0=s[:, 0:256], in1=s[:, 256:512], op=ALU.add)
-                    s = s2
-                    nb = 2
-                st[(key, c, i)] = [(s, b) for b in range(nb)]
+                st[(key, c, i)] = [(s, b) for b in range(4)]
+                if (key == "n" and 0 < c < NCH - 1) or (key == "p" and c < NCH - 1):
+                    second_add(key, c, i, nc.gpsimd)
 
         def kb(c, i, h):
             bank = mx_bank("k", c, i, h)

@@ -323,7 +323,7 @@ def tile_aftattention_kernel(tc, x, Wq, bq, Wk, bk, Wv, bv, wbias, out):
         kb(0, 1, 1)
         tq("q", 0)
         four(vb, 0)
-        perm("q", 1, "V")
+        perm("q", 1, "S")
         trw("k", 1, 0, "V")
         trw("k", 1, 1, "S")
         trw("v", 1, 0, "S")
@@ -338,11 +338,11 @@ def tile_aftattention_kernel(tc, x, Wq, bq, Wk, bk, Wv, bv, wbias, out):
         for c in range(1, NCH - 1):
             four(qb, c - 1)
             four(kb, c)
+            trw("q", c, 0)
+            trw("q", c, 1)
             batch_sum("p", c - 1, 0)
             batch_sum("p", c - 1, 1)
             wgt(c - 1)
-            trw("q", c, 0)
-            trw("q", c, 1)
             for pb in range(4):
                 ot(c - 1, pb)
             tq("q", c)

@@ -33,6 +33,7 @@ def tile_aftattention_kernel(tc, x, Wq, bq, Wk, bk, Wv, bv, wbias, out):
         accp = ctx.enter_context(tc.tile_pool(name="accp", bufs=2))
         thp = ctx.enter_context(tc.tile_pool(name="thp", bufs=10))
         outp = ctx.enter_context(tc.tile_pool(name="outp", bufs=4))
+        gop = ctx.enter_context(tc.tile_pool(name="gop", bufs=1))
         wrp = ctx.enter_context(tc.tile_pool(name="wrp", bufs=8))
         wpp = ctx.enter_context(tc.tile_pool(name="wpp", bufs=6))
         psp = ctx.enter_context(tc.psum_pool(name="psp", bufs=NPS))
@@ -43,6 +44,8 @@ def tile_aftattention_kernel(tc, x, Wq, bq, Wk, bk, Wv, bv, wbias, out):
         make_identity(nc, ident[:])
         identb = const.tile([P, P], BF16, name="identb")
         brow = const.tile([P, P], BF16, name="brow")
+        one = const.tile([P, 1], F32, name="one")
+        nc.vector.memset(one[:], 1.0)
         warm = const.tile([P, 1], F32, name="warm")
         warm2 = const.tile([P, 1], F32, name="warm2")
         bqh = const.tile([P, 8], F32, name="bqh")
@@ -264,6 +267,19 @@ def tile_aftattention_kernel(tc, x, Wq, bq, Wk, bk, Wv, bv, wbias, out):
             nc.sync.dma_start(out=out[2 * pb:2 * pb + 2, :, c * CH:(c + 1) * CH].rearrange("b t h -> t b h"),
                               in_=o[:])
 
+        def ot_ga(c, pb):
+            ot_t(c, pb)
+            g = gop.tile([P, 2, CH], F32, name="g", tag="g")
+            nc.scalar.activation(out=g[:], in_=st[("ob", c, pb)][:], func=ACT.Identity, bias=one[:], scale=1.0)
+            st[("g", c, pb)] = g
+
+        def ot_gb(c, pb):
+            o = outp.tile([P, 2, CH], F32, name="o", tag="o")
+            nc.gpsimd.tensor_tensor(out=o[:], in0=st[("g", c, pb)][:],
+                                    in1=st[("wh", c)][:].unsqueeze(1).to_broadcast([P, 2, CH]), op=ALU.mult)
+            nc.sync.dma_start(out=out[2 * pb:2 * pb + 2, :, c * CH:(c + 1) * CH].rearrange("b t h -> t b h"),
+                              in_=o[:])
+
         def ot(c, pb):
             ot_t(c, pb)
             ot_f(c, pb)
@@ -339,12 +355,14 @@ def tile_aftattention_kernel(tc, x, Wq, bq, Wk, bk, Wv, bv, wbias, out):
             four(qb, c - 1)
             four(kb, c)
             trw("q", c, 0)
-            trw("q", c, 1)
             batch_sum("p", c - 1, 0)
             batch_sum("p", c - 1, 1)
             wgt(c - 1)
-            for pb in range(4):
-                ot(c - 1, pb)
+            ot(c - 1, 0)
+            trw("q", c, 1)
+            ot(c - 1, 1)
+            ot(c - 1, 2)
+            ot(c - 1, 3)
             tq("q", c)
             perm("v", c + 1, "S")
             perm("q", c + 1, "S")
@@ -371,8 +389,11 @@ def tile_aftattention_kernel(tc, x, Wq, bq, Wk, bk, Wv, bv, wbias, out):
         batch_sum("p", c - 1, 0)
         batch_sum("p", c - 1, 1)
         wgt(c - 1)
-        for pb in range(4):
-            ot(c - 1, pb)
+        ot(c - 1, 0)
+        ot(c - 1, 1)
+        ot_ga(c - 1, 3)
+        ot(c - 1, 2)
+        ot_gb(c - 1, 3)
         four(vb, c)
         batch_sum("n", c, 0)
         batch_sum("n", c, 1)
@@ -380,10 +401,9 @@ def tile_aftattention_kernel(tc, x, Wq, bq, Wk, bk, Wv, bv, wbias, out):
         two(qb, c, 0)
         two(qb, c, 1)
         batch_sum("p", c, 0)
-        wgt(c, 0, P)
+        batch_sum("p", c, 1)
+        wgt(c)
         two(oti_t, c, 0)
         two(oti_f, c, 0)
-        batch_sum("p", c, 1)
-        wgt(c, P, CH)
         two(oti_t, c, 1)
         two(oti_f, c, 1)

from contextlib import ExitStack

import concourse.mybir as mybir
from concourse.masks import make_identity

FLOPS = 2 * 1024 * 1024 * 3072

F32 = mybir.dt.float32
BF16 = mybir.dt.bfloat16
U32 = mybir.dt.uint32
U8 = mybir.dt.uint8
FP8X4 = mybir.dt.float8_e4m3fn_x4
ACT = mybir.ActivationFunctionType
ALU = mybir.AluOpType

P = 128
B = 8
D = 1024
H = 1024
CH = 256
NCH = H // CH
NPS = 7


def tile_aftattention_kernel(tc, x, Wq, bq, Wk, bk, Wv, bv, wbias, out):
    nc = tc.nc
    with ExitStack() as ctx:
        const = ctx.enter_context(tc.tile_pool(name="const", bufs=1))
        gwp = ctx.enter_context(tc.tile_pool(name="gwp", bufs=4))
        nump = ctx.enter_context(tc.tile_pool(name="nump", bufs=8))
        prodp = ctx.enter_context(tc.tile_pool(name="prodp", bufs=6))
        addp = ctx.enter_context(tc.tile_pool(name="addp", bufs=3))
        accp = ctx.enter_context(tc.tile_pool(name="accp", bufs=2))
        thp = ctx.enter_context(tc.tile_pool(name="thp", bufs=10))
        outp = ctx.enter_context(tc.tile_pool(name="outp", bufs=4))
        gop = ctx.enter_context(tc.tile_pool(name="gop", bufs=1))
        wrp = ctx.enter_context(tc.tile_pool(name="wrp", bufs=8))
        wpp = ctx.enter_context(tc.tile_pool(name="wpp", bufs=6))
        psp = ctx.enter_context(tc.psum_pool(name="psp", bufs=NPS))
        smp = ctx.enter_context(tc.psum_pool(name="smp", bufs=1))
        ctx.enter_context(tc.manual_schedule())

        ident = const.tile([P, P], F32, name="ident")
        make_identity(nc, ident[:])
        identb = const.tile([P, P], BF16, name="identb")
        brow = const.tile([P, P], BF16, name="brow")
        one = const.tile([P, 1], F32, name="one")
        nc.vector.memset(one[:], 1.0)
        warm = const.tile([P, 1], F32, name="warm")
        warm2 = const.tile([P, 1], F32, name="warm2")
        bqh = const.tile([P, 8], F32, name="bqh")
        bvc = const.tile([P, 8], F32, name="bvc")
        zt = const.tile([P, 512], BF16, name="zt")
        nc.vector.memset(zt[:], 0.0)

        def dummy(n):
            bank = psp.tile([P, 512], F32, name="dm", tag="ps")
            for r in range(n):
                nc.tensor.matmul(out=bank[:], lhsT=zt[:, 0:P], rhs=zt[:], start=True, stop=True)

        nc.vector.memset(warm[:], 0.0)
        nc.scalar.activation(out=warm2[:], in_=warm[:], func=ACT.Exp)
        nc.vector.memset(brow[:], 0.0)
        nc.scalar.dma_start(out=brow[0:8, :], in_=bq.rearrange("(i p) -> i p", p=P))
        nc.scalar.dma_start(out=brow[8:16, :], in_=bv.rearrange("(i p) -> i p", p=P))

        x_raw = const.tile([P, B * D], BF16, name="x_raw")
        x_raw3 = x_raw[:].rearrange("p (b k) -> p b k", b=B)
        x_t = x.rearrange("b t k -> t b k")
        w_dram = {"k": Wk, "v": Wv, "q": Wq}
        w_raw = {}

        def load_x(b0, b1):
            nc.sync.dma_start(out=x_raw3[:, b0:b1, :], in_=x_t[:, b0:b1, :])

        def load_w(w, c, i0, i1):
            if i0 == 0:
                t = wrp.tile([P, 2 * D], BF16, name="wraw", tag="wraw")
                w_raw[(w, c)] = t
            nc.sync.dma_start(
                out=w_raw[(w, c)][:].rearrange("p (i k) -> p i k", i=2)[:, i0:i1, :],
                in_=w_dram[w][c * CH + i0 * P:c * CH + i1 * P, :].rearrange("(i p) k -> p i k", p=P),
            )

        load_x(0, 1)
        load_x(1, 2)
        load_x(2, 3)
        load_x(3, 4)
        load_w("k", 0, 0, 1)
        load_w("k", 0, 1, 2)
        for b in range(4, 8):
            load_x(b, b + 1)
        load_w("v", 0, 0, 2)
        load_w("q", 0, 0, 2)
        for c in range(1, NCH):
            for w in ("k", "v", "q"):
                load_w(w, c, 0, 2)

        nc.vector.tensor_copy(out=identb[:], in_=ident[:])

        def bias_stage():
            bt = psp.tile([P, P], BF16, name="bt", tag="ps")
            nc.tensor.transpose(out=bt[:], in_=brow[:], identity=identb[:])
            nc.vector.tensor_scalar_mul(out=bqh[:], in0=bt[:, 0:8], scalar1=0.5)
            nc.vector.tensor_copy(out=bvc[:], in_=bt[:, 8:16])

        xw = x_raw[:].bitcast(F32)
        gx = [const.tile([P, 2048], F32, name="gx%d" % h, align_bytes=64) for h in range(2)]
        xc = [const.tile([P, 1024], U32, name="xc%d" % h, align_bytes=256) for h in range(2)]
        xs = [const.tile([P, 1024], U8, name="xs%d" % h, align_bytes=256) for h in range(2)]

        def transpose_bank(words, first_col, sorted_words=False):
            bank = psp.tile([P, 4, P], F32, name="trb", tag="ps")
            for g in range(2):
                for u in range(2):
                    lo = first_col + 256 * g
                    if sorted_words:
                        src = words[:, lo + u * P:lo + (u + 1) * P]
                    else:
                        src = words[:, lo + u:lo + 256:2]
                    nc.tensor.transpose(out=bank[:, 2 * g + u, :], in_=src, identity=ident[:])
            return bank[:].rearrange("p (g u) r -> p g r u", g=2, u=2)

        def evac(eng, dst, src):
            if eng == "V":
                nc.vector.tensor_copy(out=dst, in_=src)
            elif eng == "G":
                nc.gpsimd.tensor_copy(out=dst, in_=src)
            else:
                nc.scalar.copy(out=dst, in_=src)

        def trx(b, eng):
            src = transpose_bank(xw, b * 512)
            dst = gx[b // 4][:].rearrange("p (g b r u) -> p g b r u", g=2, b=4, r=P, u=2)[:, :, b % 4, :, :]
            evac(eng, dst, src)

        def qx(pb):
            h = pb // 2
            for g in range(2):
                w0 = g * 512 + (pb % 2) * 256
                nc.vector.quantize_mx(out=xc[h][:, w0:w0 + 256].bitcast(FP8X4), scales=xs[h][:, w0:w0 + 256],
                                      in_=gx[h][:, 2 * w0:2 * w0 + 512].bitcast(BF16))

        wc = {}
        ws = {}
        gws = {}

        w_perm = {}

        def perm(w, c, eng, i0=0, i1=2):
            if i0 == 0:
                wp_new = wpp.tile([P, 1024], F32, name="wperm", tag="wperm")
                w_perm[(w, c)] = wp_new
            evac(eng, w_perm[(w, c)][:].rearrange("p (a u j) -> p a u j", a=4, u=2)[:, 2 * i0:2 * i1, :, :],
                 w_raw[(w, c)][:].bitcast(F32).rearrange("p (a j u) -> p a u j", a=4, u=2)[:, 2 * i0:2 * i1, :, :])

        def trw(w, c, i, eng="S"):
            if i == 0:
                gw_new = gwp.tile([P, 1024], F32, name="gw", tag="gw", align_bytes=64)
                gws[(w, c)] = gw_new
            if (w, c) in w_perm:
                src = transpose_bank(w_perm[(w, c)][:], i * 512, True)
            else:
                src = transpose_bank(w_raw[(w, c)][:].bitcast(F32), i * 512)
            dst = gws[(w, c)][:].rearrange("p (g i r u) -> p g i r u", g=2, i=2, r=P, u=2)[:, :, i, :, :]
            evac(eng, dst, src)

        def tq(w, c):
            codes_all = const.tile([P, 544], U32, name="wc_%s%d" % (w, c), align_bytes=256)
            scales_all = const.tile([P, 576], U8, name="ws_%s%d" % (w, c), align_bytes=256)
            codes = codes_all[:, 32:544]
            scales = scales_all[:, 64:576]
            nc.vector.quantize_mx(out=codes.bitcast(FP8X4), scales=scales, in_=gws[(w, c)][:].bitcast(BF16))
            wc[(w, c)] = codes
            ws[(w, c)] = scales

        def mx_bank(w, c, i, h):
            bank = psp.tile([P, 512], F32, name="mxb", tag="ps")
            for g in range(2):
                wcols = slice(g * CH + i * P, g * CH + (i + 1) * P)
                xcols = slice(g * 512, (g + 1) * 512)
                nc.tensor.matmul_mx(out=bank[:],
                                    lhsT=wc[(w, c)][:, wcols].bitcast(FP8X4), lhsT_scale=ws[(w, c)][:, wcols],
                                    rhs=xc[h][:, xcols].bitcast(FP8X4), rhs_scale=xs[h][:, xcols],
                                    start=(g == 0), stop=(g == 1))
            return bank

        st = {}

        def second_add(key, c, i, eng):
            s = st[(key, c, i)][0][0]
            s2 = addp.tile([P, 256], F32, name="r" + key, tag="r" + key)
            eng.tensor_tensor(out=s2[:], in0=s[:, 0:256], in1=s[:, 256:512], op=ALU.add)
            st[(key, c, i)] = [(s2, 0), (s2, 1)]

        def pre_add(key, c, i, h, tile):
            st[(key, c, i, h)] = tile
            if h == 1:
                s = addp.tile([P, 512], F32, name="s" + key, tag="s" + key)
                nc.gpsimd.tensor_tensor(out=s[:], in0=st[(key, c, i, 0)][:], in1=tile[:], op=ALU.add)
                st[(key, c, i)] = [(s, b) for b in range(4)]
                if (key == "n" and 0 < c < NCH - 1) or (key == "p" and c < NCH - 1):
                    second_add(key, c, i, nc.gpsimd)

        def kb(c, i, h):
            bank = mx_bank("k", c, i, h)
            n = nump.tile([P, 512], F32, name="numer", tag="numer")
            nc.scalar.activation(out=n[:], in_=bank[:], func=ACT.Exp)
            pre_add("n", c, i, h, n)

        def vb(c, i, h):
            bank = mx_bank("v", c, i, h)
            pr = prodp.tile([P, 512], F32, name="prod", tag="prod")
            nc.vector.scalar_tensor_tensor(out=pr[:], in0=bank[:], scalar=bvc[:, 2 * c + i:2 * c + i + 1],
                                           in1=st[("n", c, i, h)][:], op0=ALU.add, op1=ALU.mult)
            pre_add("p", c, i, h, pr)

        def qb(c, i, h):
            bank = mx_bank("q", c, i, h)
            t = thp.tile([P, 512], F32, name="th", tag="th")
            nc.scalar.activation(out=t[:], in_=bank[:], func=ACT.Tanh,
                                 bias=bqh[:, 2 * c + i:2 * c + i + 1], scale=0.5)
            st[("th", c, i, h)] = t

        def batch_sum(key, c, i):
            if i == 0 and key == "n":
                den_new = smp.tile([P, CH], F32, name="den", tag="den")
                st[("sum", "n", c)] = den_new
            elif i == 0:
                num_new = psp.tile([P, CH], F32, name="num", tag="ps")
                st[("sum", "p", c)] = num_new
            dst = st[("sum", key, c)][:, i * P:(i + 1) * P]
            parts = st[(key, c, i)]
            for j, (t, b) in enumerate(parts):
                nc.tensor.matmul(out=dst, lhsT=t[:, b * P:(b + 1) * P], rhs=ident[:], is_transpose=True,
                                 start=(j == 0), stop=(j == len(parts) - 1))

        def recip(c, c0=0, c1=CH):
            if c0 == 0:
                rden_new = accp.tile([P, CH], F32, name="rden", tag="rden")
                st[("rden", c)] = rden_new
            nc.vector.reciprocal(out=st[("rden", c)][:, c0:c1], in_=st[("sum", "n", c)][:, c0:c1])

        def wgt(c, c0=0, c1=CH):
            if c0 == 0:
                wh_new = accp.tile([P, CH], F32, name="wh", tag="wh")
                st[("wh", c)] = wh_new
            nc.vector.scalar_tensor_tensor(out=st[("wh", c)][:, c0:c1], in0=st[("sum", "p", c)][:, c0:c1], scalar=0.5,
                                           in1=st[("rden", c)][:, c0:c1], op0=ALU.mult, op1=ALU.mult)

        def ot_t(c, pb):
            ob = psp.tile([P, 2, CH], F32, name="ob", tag="ps")
            for bb in range(2):
                b = 2 * pb + bb
                for i in range(2):
                    nc.tensor.transpose(out=ob[:, bb, i * P:(i + 1) * P],
                                        in_=st[("th", c, i, b // 4)][:, (b % 4) * P:(b % 4 + 1) * P],
                                        identity=ident[:])
            st[("ob", c, pb)] = ob

        def ot_f(c, pb):
            ob = st[("ob", c, pb)]
            o = outp.tile([P, 2, CH], F32, name="o", tag="o")
            nc.vector.scalar_tensor_tensor(out=o[:], in0=ob[:], scalar=1.0,
                                           in1=st[("wh", c)][:].unsqueeze(1).to_broadcast([P, 2, CH]),
                                           op0=ALU.add, op1=ALU.mult)
            nc.sync.dma_start(out=out[2 * pb:2 * pb + 2, :, c * CH:(c + 1) * CH].rearrange("b t h -> t b h"),
                              in_=o[:])

        def ot_ga(c, pb):
            ot_t(c, pb)
            g = gop.tile([P, 2, CH], F32, name="g", tag="g")
            nc.scalar.activation(out=g[:], in_=st[("ob", c, pb)][:], func=ACT.Identity, bias=one[:], scale=1.0)
            st[("g", c, pb)] = g

        def ot_gb(c, pb):
            o = outp.tile([P, 2, CH], F32, name="o", tag="o")
            nc.gpsimd.tensor_tensor(out=o[:], in0=st[("g", c, pb)][:],
                                    in1=st[("wh", c)][:].unsqueeze(1).to_broadcast([P, 2, CH]), op=ALU.mult)
            nc.sync.dma_start(out=out[2 * pb:2 * pb + 2, :, c * CH:(c + 1) * CH].rearrange("b t h -> t b h"),
                              in_=o[:])

        def ot(c, pb):
            ot_t(c, pb)
            ot_f(c, pb)

        def oti_t(c, i, h):
            ob = psp.tile([P, 4, P], F32, name="obi", tag="ps")
            for b in range(4):
                nc.tensor.transpose(out=ob[:, b, :], in_=st[("th", c, i, h)][:, b * P:(b + 1) * P], identity=ident[:])
            st[("obi", c, i, h)] = ob

        def oti_f(c, i, h):
            o = outp.tile([P, 4, P], F32, name="oi", tag="o")
            nc.vector.scalar_tensor_tensor(
                out=o[:], in0=st[("obi", c, i, h)][:], scalar=1.0,
                in1=st[("wh", c)][:, i * P:(i + 1) * P].unsqueeze(1).to_broadcast([P, 4, P]),
                op0=ALU.add, op1=ALU.mult)
            h0 = c * CH + i * P
            nc.sync.dma_start(out=out[4 * h:4 * h + 4, :, h0:h0 + P].rearrange("b t h -> t b h"), in_=o[:])

        def two(f, c, i):
            f(c, i, 0)
            f(c, i, 1)

        def four(f, c):
            two(f, c, 0)
            two(f, c, 1)

        trx(0, "S")
        trx(1, "S")
        trx(2, "S")
        trx(3, "S")
        trw("k", 0, 0, "S")
        qx(0)
        trw("k", 0, 1, "S")
        trx(4, "S")
        qx(1)
        trx(5, "S")
        tq("k", 0)
        dummy(2)
        kb(0, 0, 0)
        kb(0, 1, 0)
        qx(2)
        perm("v", 0, "V")
        trx(6, "V")
        trx(7, "S")
        perm("q", 0, "V")
        qx(3)
        trw("v", 0, 0, "S")
        trw("v", 0, 1, "S")
        bias_stage()
        tq("v", 0)
        dummy(2)
        trw("q", 0, 0, "V")
        trw("q", 0, 1, "S")
        perm("k", 1, "S")
        kb(0, 0, 1)
        kb(0, 1, 1)
        tq("q", 0)
        four(vb, 0)
        perm("q", 1, "S")
        trw("k", 1, 0, "V")
        trw("k", 1, 1, "S")
        trw("v", 1, 0, "S")
        trw("v", 1, 1, "S")
        tq("k", 1)
        tq("v", 1)
        batch_sum("n", 0, 0)
        batch_sum("n", 0, 1)
        recip(0)
        perm("k", 2, "S")

        for c in range(1, NCH - 1):
            four(qb, c - 1)
            four(kb, c)
            trw("q", c, 0)
            batch_sum("p", c - 1, 0)
            batch_sum("p", c - 1, 1)
            wgt(c - 1)
            ot(c - 1, 0)
            trw("q", c, 1)
            ot(c - 1, 1)
            ot(c - 1, 2)
            ot(c - 1, 3)
            tq("q", c)
            perm("v", c + 1, "S")
            perm("q", c + 1, "S")
            if c + 2 < NCH:
                perm("k", c + 2, "S")
            four(vb, c)
            trw("k", c + 1, 0)
            trw("k", c + 1, 1)
            trw("v", c + 1, 0)
            trw("v", c + 1, 1)
            batch_sum("n", c, 0)
            batch_sum("n", c, 1)
            tq("k", c + 1)
            tq("v", c + 1)
            recip(c)
            if c == NCH - 2:
                trw("q", c + 1, 0)
                trw("q", c + 1, 1)
                tq("q", c + 1)

        c = NCH - 1
        four(qb, c - 1)
        four(kb, c)
        batch_sum("p", c - 1, 0)
        batch_sum("p", c - 1, 1)
        wgt(c - 1)
        ot(c - 1, 0)
        ot(c - 1, 1)
        ot_ga(c - 1, 3)
        ot(c - 1, 2)
        ot_gb(c - 1, 3)
        four(vb, c)
        batch_sum("n", c, 0)
        batch_sum("n", c, 1)
        recip(c)
        two(qb, c, 0)
        two(qb, c, 1)
        batch_sum("p", c, 0)
        batch_sum("p", c, 1)
        wgt(c)
        two(oti_t, c, 0)
        two(oti_f, c, 0)
        two(oti_t, c, 1)
        two(oti_f, c, 1)
